import numpy as np
import ml_dtypes


def mxq(x, axis, fmt="e4m3"):
    dtype, down = {"e4m3": (ml_dtypes.float8_e4m3fn, 7), "e5m2": (ml_dtypes.float8_e5m2, 14)}[fmt]
    v = np.moveaxis(np.asarray(x, np.float32).astype(ml_dtypes.bfloat16).astype(np.float64), axis, -1)
    blocks = v.reshape(v.shape[:-1] + (-1, 32))
    amax = np.abs(blocks).max(-1, keepdims=True)
    byte = np.maximum(np.where(amax > 0, np.frexp(amax)[1] - 1 + 127, 0) - down, 1)
    scale = np.exp2(byte - 127.0)
    codes = (blocks / scale).astype(np.float32).astype(dtype).astype(np.float64)
    return np.moveaxis((codes * scale).reshape(v.shape), -1, axis)


WIDE = False


def mx_kscale(k):
    if not WIDE:
        return np.ones(k)
    levels = np.array([10, -10, 5, -5, 0])
    a = np.random.permutation(np.resize(levels, k // 512 * 4)).reshape(k // 512, 4)
    idx = np.arange(k)
    return np.exp2(a[idx // 512, idx % 128 // 32])


BF16 = ml_dtypes.bfloat16


def bf(x):
    return np.asarray(x, np.float32).astype(BF16)


def f64(x):
    return np.asarray(x).astype(np.float64)


B, I, J, C = 512, 512, 512, 35
K = C * I
HSTEP = 2.0 / (C - 1)
PW = 6


def b_spline_cubic(x, grid):
    dist = np.abs(x[..., None] - grid) / HSTEP
    inner = 2.0 / 3.0 - dist * dist + dist * dist * dist * 0.5
    t = 2.0 - dist
    outer = t * t * t / 6.0
    return np.where(dist < 1.0, inner, np.where(dist < 2.0, outer, 0.0))


def setup_inputs():
    wide = np.abs(np.log2(mx_kscale(K))).max() > 0.0
    x = f64(bf(np.random.standard_normal((B, I))))
    w = np.random.standard_normal((I, J, C)) * 1.5 / np.sqrt(I)
    grid = bf(np.linspace(-1.0, 1.0, C) + 0.2 * HSTEP * np.random.standard_normal(C))
    u = np.random.uniform(0.5, 1.0, (B, I))
    if wide:
        g = f64(grid)
        cs = np.argmin(np.abs(g - 2.0 * HSTEP))
        edge = g[cs] - 2.0 * HSTEP
        inside = (x > edge) & (x < edge + 4.0 * HSTEP)
        x = np.where(inside, edge + HSTEP * u * 2.0 ** -PW, x)
        w[:, :, cs] *= 2.0 ** (3 * PW + 3)
    return {"x": bf(x), "spline_weight": bf(w), "grid": grid}


def reference(x, spline_weight, grid):
    x_norm = np.clip(f64(x), -0.99, 0.99)
    basis = b_spline_cubic(x_norm, f64(grid))
    bk = basis.transpose(0, 2, 1).reshape(B, K)
    wk = f64(spline_weight).transpose(2, 0, 1).reshape(K, J)
    return mxq(bk, 1, "e4m3") @ mxq(wk, 0, "e4m3")

@@ -1,0 +1,153 @@
+import math
+from contextlib import ExitStack
+
+import concourse.mybir as mybir
+from concourse.masks import make_identity
+
+F32 = mybir.dt.float32
+BF16 = mybir.dt.bfloat16
+U32 = mybir.dt.uint32
+U8 = mybir.dt.uint8
+FP8X4 = mybir.dt.float8_e4m3fn_x4
+FUNC = mybir.ActivationFunctionType
+ALU = mybir.AluOpType
+
+P = 128
+PACK = 4
+B, I, J, C = 512, 512, 512, 35
+B_TILES = B // P
+HALVES = 2
+B_HALF = B // HALVES
+HALF_COLS = B_HALF * PACK
+FLOPS = 2 * B * J * C * I
+
+H = 2.0 / (C - 1)
+REACH = 2.0 * H
+OUTER_SCALE = 1.0 / math.sqrt(6.0 * H**3)
+INNER_SCALE = 1.0 / math.sqrt(2.0 * H**3)
+
+LAG = 4
+
+
+def tile_fastkanlayer_pa_kernel(tc, x, spline_weight, grid, out):
+    nc = tc.nc
+    with ExitStack() as ctx:
+        keep = ctx.enter_context(tc.tile_pool(name="keep", bufs=1))
+        psum_acc = ctx.enter_context(tc.psum_pool(name="psum_acc", bufs=1))
+
+        w_raw = keep.tile([P, PACK, J * C], BF16)
+        x_clip = keep.tile([P, B, PACK], F32)
+        neg_grid = keep.tile([P, C], F32)
+
+        with tc.tile_pool(name="setup", bufs=1) as setup, tc.psum_pool(name="psum_x", bufs=2) as psum_x:
+            x_rows = setup.tile([P, B_TILES, I], BF16)
+            nc.sync.dma_start(out=x_rows[:], in_=x.rearrange("(m r) i -> r m i", r=P))
+            grid_bf = setup.tile([P, C], BF16)
+            nc.scalar.dma_start(out=grid_bf[:], in_=grid.partition_broadcast(P))
+            w_rows = spline_weight.rearrange("(p t) j c -> t p (j c)", t=PACK)
+            for t in range(PACK):
+                nc.sync.dma_start(out=w_raw[:, t, :], in_=w_rows[t])
+
+            nc.vector.tensor_scalar(
+                out=neg_grid[:], in0=grid_bf[:], scalar1=-1.0, scalar2=None, op0=ALU.mult
+            )
+            identity = setup.tile([P, P], F32)
+            make_identity(nc, identity[:])
+
+            for half in range(HALVES):
+                x_t = psum_x.tile([P, 2, B_HALF], F32)
+                for m in range(B_HALF // P):
+                    words = x_rows[:, half * (B_HALF // P) + m, :].bitcast(F32)
+                    words = words.rearrange("r (p u) -> r u p", u=2)
+                    for u in range(2):
+                        nc.tensor.transpose(
+                            out=x_t[:, u, m * P : (m + 1) * P], in_=words[:, u, :], identity=identity[:]
+                        )
+                pairs = x_t[:].rearrange("p u b -> p (u b)").bitcast(BF16)
+                nc.vector.tensor_scalar(
+                    out=x_clip[:, half * B_HALF : (half + 1) * B_HALF, :].rearrange(
+                        "p b (u e) -> p b u e", e=2
+                    ),
+                    in0=pairs.rearrange("p (u b e) -> p b u e", u=2, e=2),
+                    scalar1=0.99,
+                    scalar2=-0.99,
+                    op0=ALU.min,
+                    op1=ALU.max,
+                )
+
+        acc = [psum_acc.tile([P, J], F32, name="acc%d" % m) for m in range(B_TILES)]
+        x_flat = x_clip[:].rearrange("p b t -> p (b t)")
+        w_by_knot = w_raw[:].rearrange("p t (j c) -> p c j t", c=C)
+
+        with ExitStack() as loop:
+            act = loop.enter_context(tc.tile_pool(name="act", bufs=3))
+            stage = loop.enter_context(tc.tile_pool(name="stage", bufs=2))
+            b_pool = loop.enter_context(tc.tile_pool(name="b_pool", bufs=LAG + 2))
+            w_pool = loop.enter_context(tc.tile_pool(name="w_pool", bufs=2))
+
+            def basis_half(c, half, codes, scales):
+                cols = slice(half * HALF_COLS, (half + 1) * HALF_COLS)
+                dist = stage.tile([P, HALF_COLS], F32)
+                nc.scalar.activation(
+                    out=dist[:], in_=x_flat[:, cols], func=FUNC.Abs, bias=neg_grid[:, c : c + 1], scale=1.0
+                )
+                inner = act.tile([P, HALF_COLS], F32)
+                nc.scalar.activation(out=inner[:], in_=dist[:], func=FUNC.Square, scale=INNER_SCALE)
+                reach = act.tile([P, HALF_COLS], F32)
+                nc.scalar.activation(out=reach[:], in_=dist[:], func=FUNC.Relu, bias=REACH, scale=-1.0)
+                outer = act.tile([P, HALF_COLS], F32)
+                nc.scalar.activation(out=outer[:], in_=reach[:], func=FUNC.Square, scale=OUTER_SCALE)
+                nc.vector.tensor_tensor(out=outer[:], in0=reach[:], in1=outer[:], op=ALU.mult)
+                nc.vector.scalar_tensor_tensor(
+                    out=inner[:], in0=reach[:], scalar=-1.0, in1=inner[:], op0=ALU.mult, op1=ALU.mult
+                )
+                basis = stage.tile([P, HALF_COLS], BF16, align_bytes=64)
+                nc.vector.scalar_tensor_tensor(
+                    out=basis[:], in0=inner[:], scalar=2.0 / 3.0, in1=outer[:], op0=ALU.add, op1=ALU.min
+                )
+                nc.vector.quantize_mx(out=codes.bitcast(FP8X4), scales=scales, in_=basis[:])
+
+            def weights(c):
+                grouped = stage.tile([P, J, PACK], BF16, align_bytes=64)
+                nc.vector.tensor_copy(out=grouped[:], in_=w_by_knot[:, c])
+                w_codes = w_pool.tile([P, J], U32, align_bytes=64)
+                w_scales = w_pool.tile([P, J], U8, align_bytes=64)
+                nc.vector.quantize_mx(
+                    out=w_codes[:].bitcast(FP8X4),
+                    scales=w_scales[:],
+                    in_=grouped[:].rearrange("p j t -> p (j t)"),
+                )
+                return w_codes, w_scales
+
+            b_codes = {}
+            b_scales = {}
+            for c in range(C + LAG):
+                if c < C:
+                    b_codes[c] = b_pool.tile([P, B], U32, name="b_codes", align_bytes=64)
+                    b_scales[c] = b_pool.tile([P, B], U8, name="b_scales", align_bytes=64)
+                    for half in range(HALVES):
+                        rows = slice(half * B_HALF, (half + 1) * B_HALF)
+                        basis_half(c, half, b_codes[c][:, rows], b_scales[c][:, rows])
+                if c >= LAG:
+                    k = c - LAG
+                    w_codes, w_scales = weights(k)
+                    for m in range(B_TILES):
+                        rows = slice(m * P, (m + 1) * P)
+                        nc.tensor.matmul_mx(
+                            out=acc[m][:],
+                            lhsT=b_codes[k][:, rows].bitcast(FP8X4),
+                            lhsT_scale=b_scales[k][:, rows],
+                            rhs=w_codes[:].bitcast(FP8X4),
+                            rhs_scale=w_scales[:],
+                            start=(k == 0),
+                            stop=(k == C - 1),
+                        )
+
+        with tc.tile_pool(name="result", bufs=B_TILES) as result:
+            for m in range(B_TILES):
+                out_rows = result.tile([P, J], F32)
+                if m % 2 == 0:
+                    nc.scalar.copy(out=out_rows[:], in_=acc[m][:])
+                else:
+                    nc.vector.tensor_copy(out=out_rows[:], in_=acc[m][:])
+                nc.sync.dma_start(out=out[m * P : (m + 1) * P, :], in_=out_rows[:])

@@ -84,64 +84,93 @@ def tile_fastkanlayer_pa_kernel(tc, x, spline_weight, grid, out):
             stage = loop.enter_context(tc.tile_pool(name="stage", bufs=2))
             b_pool = loop.enter_context(tc.tile_pool(name="b_pool", bufs=LAG + 2))
             w_pool = loop.enter_context(tc.tile_pool(name="w_pool", bufs=2))
+            loop.enter_context(tc.manual_schedule())
 
-            def basis_half(c, half, codes, scales):
-                cols = slice(half * HALF_COLS, (half + 1) * HALF_COLS)
-                dist = stage.tile([P, HALF_COLS], F32)
+            dist, reach, inner, outer, basis = {}, {}, {}, {}, {}
+            b_codes, b_scales, grouped, w_codes, w_scales = {}, {}, {}, {}, {}
+
+            def distance(n):
+                cols = slice((n % HALVES) * HALF_COLS, (n % HALVES + 1) * HALF_COLS)
+                c = n // HALVES
+                dist[n] = stage.tile([P, HALF_COLS], F32, name="dist")
                 nc.scalar.activation(
-                    out=dist[:], in_=x_flat[:, cols], func=FUNC.Abs, bias=neg_grid[:, c : c + 1], scale=1.0
+                    out=dist[n][:], in_=x_flat[:, cols], func=FUNC.Abs, bias=neg_grid[:, c : c + 1], scale=1.0
                 )
-                inner = act.tile([P, HALF_COLS], F32)
-                nc.scalar.activation(out=inner[:], in_=dist[:], func=FUNC.Square, scale=INNER_SCALE)
-                reach = act.tile([P, HALF_COLS], F32)
-                nc.scalar.activation(out=reach[:], in_=dist[:], func=FUNC.Relu, bias=REACH, scale=-1.0)
-                outer = act.tile([P, HALF_COLS], F32)
-                nc.scalar.activation(out=outer[:], in_=reach[:], func=FUNC.Square, scale=OUTER_SCALE)
-                nc.vector.tensor_tensor(out=outer[:], in0=reach[:], in1=outer[:], op=ALU.mult)
-                nc.vector.scalar_tensor_tensor(
-                    out=inner[:], in0=reach[:], scalar=-1.0, in1=inner[:], op0=ALU.mult, op1=ALU.mult
-                )
-                basis = stage.tile([P, HALF_COLS], BF16, align_bytes=64)
-                nc.vector.scalar_tensor_tensor(
-                    out=basis[:], in0=inner[:], scalar=2.0 / 3.0, in1=outer[:], op0=ALU.add, op1=ALU.min
-                )
-                nc.vector.quantize_mx(out=codes.bitcast(FP8X4), scales=scales, in_=basis[:])
 
-            def weights(c):
-                grouped = stage.tile([P, J, PACK], BF16, align_bytes=64)
-                nc.vector.tensor_copy(out=grouped[:], in_=w_by_knot[:, c])
-                w_codes = w_pool.tile([P, J], U32, align_bytes=64)
-                w_scales = w_pool.tile([P, J], U8, align_bytes=64)
-                nc.vector.quantize_mx(
-                    out=w_codes[:].bitcast(FP8X4),
-                    scales=w_scales[:],
-                    in_=grouped[:].rearrange("p j t -> p (j t)"),
-                )
-                return w_codes, w_scales
+            def factors(n):
+                reach[n] = act.tile([P, HALF_COLS], F32, name="reach")
+                nc.scalar.activation(out=reach[n][:], in_=dist[n][:], func=FUNC.Relu, bias=REACH, scale=-1.0)
+                inner[n] = act.tile([P, HALF_COLS], F32, name="inner")
+                nc.scalar.activation(out=inner[n][:], in_=dist[n][:], func=FUNC.Square, scale=INNER_SCALE)
+                outer[n] = act.tile([P, HALF_COLS], F32, name="outer")
+                nc.scalar.activation(out=outer[n][:], in_=reach[n][:], func=FUNC.Square, scale=OUTER_SCALE)
 
-            b_codes = {}
-            b_scales = {}
-            for c in range(C + LAG):
-                if c < C:
+            def products(n):
+                nc.vector.tensor_tensor(out=outer[n][:], in0=reach[n][:], in1=outer[n][:], op=ALU.mult)
+                nc.vector.scalar_tensor_tensor(
+                    out=inner[n][:], in0=reach[n][:], scalar=-1.0, in1=inner[n][:], op0=ALU.mult, op1=ALU.mult
+                )
+
+            def smaller(n):
+                basis[n] = stage.tile([P, HALF_COLS], BF16, name="basis", align_bytes=64)
+                nc.vector.scalar_tensor_tensor(
+                    out=basis[n][:], in0=inner[n][:], scalar=2.0 / 3.0, in1=outer[n][:], op0=ALU.add, op1=ALU.min
+                )
+
+            def quantise_basis(n):
+                c = n // HALVES
+                rows = slice((n % HALVES) * B_HALF, (n % HALVES + 1) * B_HALF)
+                if n % HALVES == 0:
                     b_codes[c] = b_pool.tile([P, B], U32, name="b_codes", align_bytes=64)
                     b_scales[c] = b_pool.tile([P, B], U8, name="b_scales", align_bytes=64)
-                    for half in range(HALVES):
-                        rows = slice(half * B_HALF, (half + 1) * B_HALF)
-                        basis_half(c, half, b_codes[c][:, rows], b_scales[c][:, rows])
-                if c >= LAG:
-                    k = c - LAG
-                    w_codes, w_scales = weights(k)
-                    for m in range(B_TILES):
-                        rows = slice(m * P, (m + 1) * P)
-                        nc.tensor.matmul_mx(
-                            out=acc[m][:],
-                            lhsT=b_codes[k][:, rows].bitcast(FP8X4),
-                            lhsT_scale=b_scales[k][:, rows],
-                            rhs=w_codes[:].bitcast(FP8X4),
-                            rhs_scale=w_scales[:],
-                            start=(k == 0),
-                            stop=(k == C - 1),
-                        )
+                nc.vector.quantize_mx(
+                    out=b_codes[c][:, rows].bitcast(FP8X4), scales=b_scales[c][:, rows], in_=basis[n][:]
+                )
+
+            def group_weights(k):
+                grouped[k] = stage.tile([P, J, PACK], BF16, name="grouped", align_bytes=64)
+                nc.vector.tensor_copy(out=grouped[k][:], in_=w_by_knot[:, k])
+
+            def quantise_weights(k):
+                w_codes[k] = w_pool.tile([P, J], U32, name="w_codes", align_bytes=64)
+                w_scales[k] = w_pool.tile([P, J], U8, name="w_scales", align_bytes=64)
+                nc.vector.quantize_mx(
+                    out=w_codes[k][:].bitcast(FP8X4),
+                    scales=w_scales[k][:],
+                    in_=grouped[k][:].rearrange("p j t -> p (j t)"),
+                )
+
+            def multiply(k):
+                for m in range(B_TILES):
+                    rows = slice(m * P, (m + 1) * P)
+                    nc.tensor.matmul_mx(
+                        out=acc[m][:],
+                        lhsT=b_codes[k][:, rows].bitcast(FP8X4),
+                        lhsT_scale=b_scales[k][:, rows],
+                        rhs=w_codes[k][:].bitcast(FP8X4),
+                        rhs_scale=w_scales[k][:],
+                        start=(k == 0),
+                        stop=(k == C - 1),
+                    )
+
+            units = C * HALVES
+            distance(0)
+            for n in range(units + LAG * HALVES + 1):
+                if n + 1 < units:
+                    distance(n + 1)
+                if n < units:
+                    factors(n)
+                    products(n)
+                if 1 <= n <= units:
+                    quantise_basis(n - 1)
+                if n < units:
+                    smaller(n)
+                k = n // HALVES - LAG
+                if 0 <= k < C and n % HALVES == 0:
+                    group_weights(k)
+                if 0 <= k < C and n % HALVES == 1:
+                    quantise_weights(k)
+                    multiply(k)
 
         with tc.tile_pool(name="result", bufs=B_TILES) as result:
             for m in range(B_TILES):

@@ -27,6 +27,7 @@ OUTER_SCALE = 1.0 / math.sqrt(6.0 * H**3)
 INNER_SCALE = 1.0 / math.sqrt(2.0 * H**3)
 
 LAG = 4
+GROUP = 4
 
 
 def tile_fastkanlayer_pa_kernel(tc, x, spline_weight, grid, out):
@@ -77,13 +78,14 @@ def tile_fastkanlayer_pa_kernel(tc, x, spline_weight, grid, out):
 
         acc = [psum_acc.tile([P, J], F32, name="acc%d" % m) for m in range(B_TILES)]
         x_flat = x_clip[:].rearrange("p b t -> p (b t)")
-        w_by_knot = w_raw[:].rearrange("p t (j c) -> p c j t", c=C)
+        w_view = w_raw[:].rearrange("p t (j c) -> p j t c", c=C)
 
         with ExitStack() as loop:
             act = loop.enter_context(tc.tile_pool(name="act", bufs=3))
             stage = loop.enter_context(tc.tile_pool(name="stage", bufs=2))
             b_pool = loop.enter_context(tc.tile_pool(name="b_pool", bufs=LAG + 2))
             w_pool = loop.enter_context(tc.tile_pool(name="w_pool", bufs=2))
+            g_pool = loop.enter_context(tc.tile_pool(name="g_pool", bufs=1))
             loop.enter_context(tc.manual_schedule())
 
             dist, reach, inner, outer, basis = {}, {}, {}, {}, {}
@@ -127,9 +129,16 @@ def tile_fastkanlayer_pa_kernel(tc, x, spline_weight, grid, out):
                     out=b_codes[c][:, rows].bitcast(FP8X4), scales=b_scales[c][:, rows], in_=basis[n][:]
                 )
 
-            def group_weights(k):
-                grouped[k] = stage.tile([P, J, PACK], BF16, name="grouped", align_bytes=64)
-                nc.vector.tensor_copy(out=grouped[k][:], in_=w_by_knot[:, k])
+            def group_weights(g, half):
+                first = g * GROUP
+                count = min(GROUP, C - first)
+                js = slice(half * (J // HALVES), (half + 1) * (J // HALVES))
+                if half == 0:
+                    grouped[g] = g_pool.tile([P, GROUP, J, PACK], BF16, name="grouped", align_bytes=64)
+                nc.vector.tensor_copy(
+                    out=grouped[g][:, 0:count, js, :].rearrange("p c j t -> p j t c"),
+                    in_=w_view[:, js, :, first : first + count],
+                )
 
             def quantise_weights(k):
                 w_codes[k] = w_pool.tile([P, J], U32, name="w_codes", align_bytes=64)
@@ -137,7 +146,7 @@ def tile_fastkanlayer_pa_kernel(tc, x, spline_weight, grid, out):
                 nc.vector.quantize_mx(
                     out=w_codes[k][:].bitcast(FP8X4),
                     scales=w_scales[k][:],
-                    in_=grouped[k][:].rearrange("p j t -> p (j t)"),
+                    in_=grouped[k // GROUP][:, k % GROUP, :, :].rearrange("p j t -> p (j t)"),
                 )
 
             def multiply(k):
@@ -156,8 +165,12 @@ def tile_fastkanlayer_pa_kernel(tc, x, spline_weight, grid, out):
             units = C * HALVES
             distance(0)
             for n in range(units + LAG * HALVES + 1):
+                g, step = divmod(n - LAG * HALVES, GROUP * HALVES)
+                k = g * GROUP + step // HALVES
                 if n + 1 < units:
                     distance(n + 1)
+                if 0 <= g * GROUP < C and step < HALVES:
+                    group_weights(g, step)
                 if n < units:
                     factors(n)
                     products(n)
@@ -165,10 +178,7 @@ def tile_fastkanlayer_pa_kernel(tc, x, spline_weight, grid, out):
                     quantise_basis(n - 1)
                 if n < units:
                     smaller(n)
-                k = n // HALVES - LAG
-                if 0 <= k < C and n % HALVES == 0:
-                    group_weights(k)
-                if 0 <= k < C and n % HALVES == 1:
+                if 0 <= k < C and step % HALVES == 1:
                     quantise_weights(k)
                     multiply(k)
 

@@ -24,10 +24,12 @@ FLOPS = 2 * B * J * C * I
 H = 2.0 / (C - 1)
 REACH = 2.0 * H
 OUTER_SCALE = 1.0 / math.sqrt(6.0 * H**3)
-INNER_SCALE = 1.0 / math.sqrt(2.0 * H**3)
+INNER_SCALE = math.sqrt(2.0 / (3.0 * H**3))
 
 LAG = 4
 GROUP = 4
+PIECES = GROUP * HALVES
+J_PIECE = J // PIECES
 
 
 def tile_fastkanlayer_pa_kernel(tc, x, spline_weight, grid, out):
@@ -83,41 +85,46 @@ def tile_fastkanlayer_pa_kernel(tc, x, spline_weight, grid, out):
         with ExitStack() as loop:
             act = loop.enter_context(tc.tile_pool(name="act", bufs=3))
             stage = loop.enter_context(tc.tile_pool(name="stage", bufs=2))
-            b_pool = loop.enter_context(tc.tile_pool(name="b_pool", bufs=LAG + 2))
-            w_pool = loop.enter_context(tc.tile_pool(name="w_pool", bufs=2))
-            g_pool = loop.enter_context(tc.tile_pool(name="g_pool", bufs=1))
+            b_pool = loop.enter_context(tc.tile_pool(name="b_pool", bufs=LAG + 1))
             loop.enter_context(tc.manual_schedule())
 
-            dist, reach, inner, outer, basis = {}, {}, {}, {}, {}
+            dist, inner, outer, basis = {}, {}, {}, {}
             b_codes, b_scales, grouped, w_codes, w_scales = {}, {}, {}, {}, {}
 
             def distance(n):
                 cols = slice((n % HALVES) * HALF_COLS, (n % HALVES + 1) * HALF_COLS)
                 c = n // HALVES
-                dist[n] = stage.tile([P, HALF_COLS], F32, name="dist")
+                dist[n] = act.tile([P, HALF_COLS], F32, name="dist")
                 nc.scalar.activation(
                     out=dist[n][:], in_=x_flat[:, cols], func=FUNC.Abs, bias=neg_grid[:, c : c + 1], scale=1.0
                 )
 
-            def factors(n):
-                reach[n] = act.tile([P, HALF_COLS], F32, name="reach")
-                nc.scalar.activation(out=reach[n][:], in_=dist[n][:], func=FUNC.Relu, bias=REACH, scale=-1.0)
-                inner[n] = act.tile([P, HALF_COLS], F32, name="inner")
-                nc.scalar.activation(out=inner[n][:], in_=dist[n][:], func=FUNC.Square, scale=INNER_SCALE)
+            def squares(n):
                 outer[n] = act.tile([P, HALF_COLS], F32, name="outer")
-                nc.scalar.activation(out=outer[n][:], in_=reach[n][:], func=FUNC.Square, scale=OUTER_SCALE)
-
-            def products(n):
-                nc.vector.tensor_tensor(out=outer[n][:], in0=reach[n][:], in1=outer[n][:], op=ALU.mult)
-                nc.vector.scalar_tensor_tensor(
-                    out=inner[n][:], in0=reach[n][:], scalar=-1.0, in1=inner[n][:], op0=ALU.mult, op1=ALU.mult
+                nc.scalar.activation(
+                    out=outer[n][:], in_=dist[n][:], func=FUNC.Square, bias=OUTER_SCALE * REACH, scale=-OUTER_SCALE
+                )
+                inner[n] = act.tile([P, HALF_COLS], F32, name="inner")
+                nc.scalar.activation(
+                    out=inner[n][:], in_=dist[n][:], func=FUNC.Square, bias=INNER_SCALE * H, scale=-INNER_SCALE
                 )
 
-            def smaller(n):
+            def cubes(n):
+                nc.vector.scalar_tensor_tensor(
+                    out=outer[n][:], in0=dist[n][:], scalar=REACH, in1=outer[n][:], op0=ALU.subtract, op1=ALU.mult
+                )
+                nc.vector.scalar_tensor_tensor(
+                    out=inner[n][:], in0=dist[n][:], scalar=H, in1=inner[n][:], op0=ALU.subtract, op1=ALU.mult
+                )
+
+            def difference(n):
                 basis[n] = stage.tile([P, HALF_COLS], BF16, name="basis", align_bytes=64)
                 nc.vector.scalar_tensor_tensor(
-                    out=basis[n][:], in0=inner[n][:], scalar=2.0 / 3.0, in1=outer[n][:], op0=ALU.add, op1=ALU.min
+                    out=basis[n][:], in0=inner[n][:], scalar=0.0, in1=outer[n][:], op0=ALU.min, op1=ALU.subtract
                 )
+
+            def no_negatives(n):
+                nc.vector.tensor_scalar_max(out=basis[n][:], in0=basis[n][:], scalar1=0.0)
 
             def quantise_basis(n):
                 c = n // HALVES
@@ -129,20 +136,19 @@ def tile_fastkanlayer_pa_kernel(tc, x, spline_weight, grid, out):
                     out=b_codes[c][:, rows].bitcast(FP8X4), scales=b_scales[c][:, rows], in_=basis[n][:]
                 )
 
-            def group_weights(g, half):
+            def weight_views(g, first_j, last_j):
                 first = g * GROUP
                 count = min(GROUP, C - first)
-                js = slice(half * (J // HALVES), (half + 1) * (J // HALVES))
-                if half == 0:
-                    grouped[g] = g_pool.tile([P, GROUP, J, PACK], BF16, name="grouped", align_bytes=64)
-                nc.vector.tensor_copy(
-                    out=grouped[g][:, 0:count, js, :].rearrange("p c j t -> p j t c"),
-                    in_=w_view[:, js, :, first : first + count],
+                if first_j == 0:
+                    grouped[g] = stage.tile([P, GROUP, J, PACK], BF16, name="grouped", align_bytes=64)
+                return (
+                    grouped[g][:, 0:count, first_j:last_j, :].rearrange("p c j t -> p j t c"),
+                    w_view[:, first_j:last_j, :, first : first + count],
                 )
 
             def quantise_weights(k):
-                w_codes[k] = w_pool.tile([P, J], U32, name="w_codes", align_bytes=64)
-                w_scales[k] = w_pool.tile([P, J], U8, name="w_scales", align_bytes=64)
+                w_codes[k] = stage.tile([P, J], U32, name="w_codes", align_bytes=64)
+                w_scales[k] = stage.tile([P, J], U8, name="w_scales", align_bytes=64)
                 nc.vector.quantize_mx(
                     out=w_codes[k][:].bitcast(FP8X4),
                     scales=w_scales[k][:],
@@ -165,19 +171,27 @@ def tile_fastkanlayer_pa_kernel(tc, x, spline_weight, grid, out):
             units = C * HALVES
             distance(0)
             for n in range(units + LAG * HALVES + 1):
-                g, step = divmod(n - LAG * HALVES, GROUP * HALVES)
+                g, step = divmod(n - LAG * HALVES, PIECES)
                 k = g * GROUP + step // HALVES
                 if n + 1 < units:
                     distance(n + 1)
-                if 0 <= g * GROUP < C and step < HALVES:
-                    group_weights(g, step)
                 if n < units:
-                    factors(n)
-                    products(n)
+                    squares(n)
+                if g == -1 and step >= PIECES - HALVES:
+                    half = step - (PIECES - HALVES)
+                    to_view, from_view = weight_views(0, half * (J // HALVES), (half + 1) * (J // HALVES))
+                    nc.vector.tensor_copy(out=to_view, in_=from_view)
+                if g >= 0 and (g + 1) * GROUP < C:
+                    to_view, from_view = weight_views(g + 1, step * J_PIECE, (step + 1) * J_PIECE)
+                    nc.scalar.copy(out=to_view, in_=from_view)
+                if n < units:
+                    cubes(n)
+                if 1 <= n <= units:
+                    no_negatives(n - 1)
+                if n < units:
+                    difference(n)
                 if 1 <= n <= units:
                     quantise_basis(n - 1)
-                if n < units:
-                    smaller(n)
                 if 0 <= k < C and step % HALVES == 1:
                     quantise_weights(k)
                     multiply(k)

@@ -26,10 +26,12 @@ REACH = 2.0 * H
 OUTER_SCALE = 1.0 / math.sqrt(6.0 * H**3)
 INNER_SCALE = math.sqrt(2.0 / (3.0 * H**3))
 
-LAG = 4
+LAG = 5
 GROUP = 4
 PIECES = GROUP * HALVES
 J_PIECE = J // PIECES
+SCALAR_PIECES = 7
+LEAD = 2
 
 
 def tile_fastkanlayer_pa_kernel(tc, x, spline_weight, grid, out):
@@ -43,6 +45,9 @@ def tile_fastkanlayer_pa_kernel(tc, x, spline_weight, grid, out):
         neg_grid = keep.tile([P, C], F32)
 
         with tc.tile_pool(name="setup", bufs=1) as setup, tc.psum_pool(name="psum_x", bufs=2) as psum_x:
+            warm = setup.tile([P, 1], F32)
+            nc.vector.memset(warm[:], 0.0)
+            nc.scalar.activation(out=warm[:], in_=warm[:], func=FUNC.Abs)
             x_rows = setup.tile([P, B_TILES, I], BF16)
             nc.sync.dma_start(out=x_rows[:], in_=x.rearrange("(m r) i -> r m i", r=P))
             grid_bf = setup.tile([P, C], BF16)
@@ -83,9 +88,9 @@ def tile_fastkanlayer_pa_kernel(tc, x, spline_weight, grid, out):
         w_view = w_raw[:].rearrange("p t (j c) -> p j t c", c=C)
 
         with ExitStack() as loop:
-            act = loop.enter_context(tc.tile_pool(name="act", bufs=3))
+            act = loop.enter_context(tc.tile_pool(name="act", bufs=LEAD + 1))
             stage = loop.enter_context(tc.tile_pool(name="stage", bufs=2))
-            b_pool = loop.enter_context(tc.tile_pool(name="b_pool", bufs=LAG + 1))
+            b_pool = loop.enter_context(tc.tile_pool(name="b_pool", bufs=LAG * HALVES + 1))
             loop.enter_context(tc.manual_schedule())
 
             dist, inner, outer, basis = {}, {}, {}, {}
@@ -127,14 +132,9 @@ def tile_fastkanlayer_pa_kernel(tc, x, spline_weight, grid, out):
                 nc.vector.tensor_scalar_max(out=basis[n][:], in0=basis[n][:], scalar1=0.0)
 
             def quantise_basis(n):
-                c = n // HALVES
-                rows = slice((n % HALVES) * B_HALF, (n % HALVES + 1) * B_HALF)
-                if n % HALVES == 0:
-                    b_codes[c] = b_pool.tile([P, B], U32, name="b_codes", align_bytes=64)
-                    b_scales[c] = b_pool.tile([P, B], U8, name="b_scales", align_bytes=64)
-                nc.vector.quantize_mx(
-                    out=b_codes[c][:, rows].bitcast(FP8X4), scales=b_scales[c][:, rows], in_=basis[n][:]
-                )
+                b_codes[n] = b_pool.tile([P, B_HALF], U32, name="b_codes", align_bytes=64)
+                b_scales[n] = b_pool.tile([P, B_HALF], U8, name="b_scales", align_bytes=64)
+                nc.vector.quantize_mx(out=b_codes[n][:].bitcast(FP8X4), scales=b_scales[n][:], in_=basis[n][:])
 
             def weight_views(g, first_j, last_j):
                 first = g * GROUP
@@ -157,11 +157,12 @@ def tile_fastkanlayer_pa_kernel(tc, x, spline_weight, grid, out):
 
             def multiply(k):
                 for m in range(B_TILES):
-                    rows = slice(m * P, (m + 1) * P)
+                    n = k * HALVES + m * P // B_HALF
+                    rows = slice(m * P % B_HALF, m * P % B_HALF + P)
                     nc.tensor.matmul_mx(
                         out=acc[m][:],
-                        lhsT=b_codes[k][:, rows].bitcast(FP8X4),
-                        lhsT_scale=b_scales[k][:, rows],
+                        lhsT=b_codes[n][:, rows].bitcast(FP8X4),
+                        lhsT_scale=b_scales[n][:, rows],
                         rhs=w_codes[k][:].bitcast(FP8X4),
                         rhs_scale=w_scales[k][:],
                         start=(k == 0),
@@ -181,9 +182,13 @@ def tile_fastkanlayer_pa_kernel(tc, x, spline_weight, grid, out):
                     half = step - (PIECES - HALVES)
                     to_view, from_view = weight_views(0, half * (J // HALVES), (half + 1) * (J // HALVES))
                     nc.vector.tensor_copy(out=to_view, in_=from_view)
-                if g >= 0 and (g + 1) * GROUP < C:
-                    to_view, from_view = weight_views(g + 1, step * J_PIECE, (step + 1) * J_PIECE)
-                    nc.scalar.copy(out=to_view, in_=from_view)
+                ahead, piece = divmod(n - LAG * HALVES - LEAD, PIECES)
+                if ahead >= 0 and (ahead + 1) * GROUP < C:
+                    to_view, from_view = weight_views(ahead + 1, piece * J_PIECE, (piece + 1) * J_PIECE)
+                    if piece < SCALAR_PIECES:
+                        nc.scalar.copy(out=to_view, in_=from_view)
+                    else:
+                        nc.vector.tensor_copy(out=to_view, in_=from_view)
                 if n < units:
                     cubes(n)
                 if 1 <= n <= units:

@@ -6,6 +6,7 @@ from concourse.masks import make_identity
 
 F32 = mybir.dt.float32
 BF16 = mybir.dt.bfloat16
+I32 = mybir.dt.int32
 U32 = mybir.dt.uint32
 U8 = mybir.dt.uint8
 FP8X4 = mybir.dt.float8_e4m3fn_x4
@@ -18,6 +19,7 @@ B, I, J, C = 512, 512, 512, 35
 B_TILES = B // P
 HALVES = 2
 B_HALF = B // HALVES
+M_HALF = B_HALF // P
 HALF_COLS = B_HALF * PACK
 FLOPS = 2 * B * J * C * I
 
@@ -26,90 +28,92 @@ REACH = 2.0 * H
 OUTER_SCALE = 1.0 / math.sqrt(6.0 * H**3)
 INNER_SCALE = math.sqrt(2.0 / (3.0 * H**3))
 
-LAG = 5
+CLASSES = 7
+MEMBERS = C // CLASSES
+SHARE = 2
+SETS = -(-CLASSES // SHARE)
+EARLY = 4
+
 GROUP = 4
-PIECES = GROUP * HALVES
+PIECES = 4
 J_PIECE = J // PIECES
-SCALAR_PIECES = 7
-LEAD = 2
 
 
 def tile_fastkanlayer_pa_kernel(tc, x, spline_weight, grid, out):
     nc = tc.nc
     with ExitStack() as ctx:
-        keep = ctx.enter_context(tc.tile_pool(name="keep", bufs=1))
+        keep = ctx.enter_context(tc.tile_pool(name="keep", bufs=1, side="left"))
         psum_acc = ctx.enter_context(tc.psum_pool(name="psum_acc", bufs=1))
 
         w_raw = keep.tile([P, PACK, J * C], BF16)
-        x_clip = keep.tile([P, B, PACK], F32)
         neg_grid = keep.tile([P, C], F32)
+        steps = keep.tile([P, C], F32)
+        identity = keep.tile([P, P], F32)
+        member = [keep.tile([P, B, PACK], BF16, name="member%d" % s) for s in range(SETS)]
+        value = [keep.tile([P, B, PACK], BF16, name="value%d" % r) for r in range(EARLY)]
 
-        with tc.tile_pool(name="setup", bufs=1) as setup, tc.psum_pool(name="psum_x", bufs=2) as psum_x:
-            warm = setup.tile([P, 1], F32)
-            nc.vector.memset(warm[:], 0.0)
-            nc.scalar.activation(out=warm[:], in_=warm[:], func=FUNC.Abs)
-            x_rows = setup.tile([P, B_TILES, I], BF16)
-            nc.sync.dma_start(out=x_rows[:], in_=x.rearrange("(m r) i -> r m i", r=P))
-            grid_bf = setup.tile([P, C], BF16)
-            nc.scalar.dma_start(out=grid_bf[:], in_=grid.partition_broadcast(P))
-            w_rows = spline_weight.rearrange("(p t) j c -> t p (j c)", t=PACK)
-            for t in range(PACK):
-                nc.sync.dma_start(out=w_raw[:, t, :], in_=w_rows[t])
+        with ExitStack() as first:
+            wide = first.enter_context(tc.tile_pool(name="wide", bufs=1, side="right"))
+            step_pool = first.enter_context(tc.tile_pool(name="step_pool", bufs=10, side="right"))
+            act = first.enter_context(tc.tile_pool(name="act", bufs=2, side="right"))
+            psum_u = first.enter_context(tc.psum_pool(name="psum_u", bufs=4))
 
-            nc.vector.tensor_scalar(
-                out=neg_grid[:], in0=grid_bf[:], scalar1=-1.0, scalar2=None, op0=ALU.mult
-            )
-            identity = setup.tile([P, P], F32)
-            make_identity(nc, identity[:])
+            x_rows_clip = wide.tile([P, B_TILES, PACK, P], F32)
 
-            for half in range(HALVES):
-                x_t = psum_x.tile([P, 2, B_HALF], F32)
-                for m in range(B_HALF // P):
-                    words = x_rows[:, half * (B_HALF // P) + m, :].bitcast(F32)
-                    words = words.rearrange("r (p u) -> r u p", u=2)
-                    for u in range(2):
-                        nc.tensor.transpose(
-                            out=x_t[:, u, m * P : (m + 1) * P], in_=words[:, u, :], identity=identity[:]
+            pieces, dist, inner, outer = {}, {}, {}, {}
+
+            def border(r, k):
+                return -1.0 + H * (CLASSES * k + r - r % SHARE - 3)
+
+            def moves(n):
+                r, half = divmod(n, HALVES)
+                for m in range(half * M_HALF, (half + 1) * M_HALF):
+                    for k in range(1, MEMBERS):
+                        c = r + CLASSES * k
+                        pieces[r, m, k] = step_pool.tile([P, PACK, P], F32, name="piece")
+                        nc.vector.tensor_scalar(
+                            out=pieces[r, m, k][:],
+                            in0=x_rows_clip[:, m, :, :],
+                            scalar1=border(r, k),
+                            scalar2=steps[:, c : c + 1],
+                            op0=ALU.is_ge,
+                            op1=ALU.mult,
                         )
-                pairs = x_t[:].rearrange("p u b -> p (u b)").bitcast(BF16)
-                nc.vector.tensor_scalar(
-                    out=x_clip[:, half * B_HALF : (half + 1) * B_HALF, :].rearrange(
-                        "p b (u e) -> p b u e", e=2
-                    ),
-                    in0=pairs.rearrange("p (u b e) -> p b u e", u=2, e=2),
-                    scalar1=0.99,
-                    scalar2=-0.99,
-                    op0=ALU.min,
-                    op1=ALU.max,
-                )
 
-        acc = [psum_acc.tile([P, J], F32, name="acc%d" % m) for m in range(B_TILES)]
-        x_flat = x_clip[:].rearrange("p b t -> p (b t)")
-        w_view = w_raw[:].rearrange("p t (j c) -> p j t c", c=C)
-
-        with ExitStack() as loop:
-            act = loop.enter_context(tc.tile_pool(name="act", bufs=LEAD + 1))
-            stage = loop.enter_context(tc.tile_pool(name="stage", bufs=2))
-            b_pool = loop.enter_context(tc.tile_pool(name="b_pool", bufs=LAG * HALVES + 1))
-            loop.enter_context(tc.manual_schedule())
-
-            dist, inner, outer, basis = {}, {}, {}, {}
-            b_codes, b_scales, grouped, w_codes, w_scales = {}, {}, {}, {}, {}
+            def turn(parts):
+                turned = psum_u.tile([P, PACK, P], F32, name="turned")
+                for t in range(PACK):
+                    for i, part in enumerate(parts):
+                        nc.tensor.matmul(
+                            out=turned[:, t, :],
+                            lhsT=part[:, t, :],
+                            rhs=identity[:],
+                            is_transpose=True,
+                            start=(i == 0),
+                            stop=(i == len(parts) - 1),
+                        )
+                return turned[:].rearrange("p t r -> p r t")
 
             def distance(n):
-                cols = slice((n % HALVES) * HALF_COLS, (n % HALVES + 1) * HALF_COLS)
-                c = n // HALVES
-                dist[n] = act.tile([P, HALF_COLS], F32, name="dist")
-                nc.scalar.activation(
-                    out=dist[n][:], in_=x_flat[:, cols], func=FUNC.Abs, bias=neg_grid[:, c : c + 1], scale=1.0
-                )
+                r, half = divmod(n, HALVES)
+                dist[n] = act.tile([P, B_HALF, PACK], F32, name="dist")
+                for m in range(M_HALF):
+                    mm = half * M_HALF + m
+                    signed = turn([x_rows_clip[:, mm, :, :]] + [pieces[r, mm, k] for k in range(1, MEMBERS)])
+                    nc.scalar.activation(
+                        out=dist[n][:, m * P : (m + 1) * P, :],
+                        in_=signed,
+                        func=FUNC.Abs,
+                        bias=neg_grid[:, r : r + 1],
+                        scale=1.0,
+                    )
 
             def squares(n):
-                outer[n] = act.tile([P, HALF_COLS], F32, name="outer")
+                outer[n] = act.tile([P, B_HALF, PACK], F32, name="outer")
                 nc.scalar.activation(
                     out=outer[n][:], in_=dist[n][:], func=FUNC.Square, bias=OUTER_SCALE * REACH, scale=-OUTER_SCALE
                 )
-                inner[n] = act.tile([P, HALF_COLS], F32, name="inner")
+                inner[n] = act.tile([P, B_HALF, PACK], F32, name="inner")
                 nc.scalar.activation(
                     out=inner[n][:], in_=dist[n][:], func=FUNC.Square, bias=INNER_SCALE * H, scale=-INNER_SCALE
                 )
@@ -122,86 +126,194 @@ def tile_fastkanlayer_pa_kernel(tc, x, spline_weight, grid, out):
                     out=inner[n][:], in0=dist[n][:], scalar=H, in1=inner[n][:], op0=ALU.subtract, op1=ALU.mult
                 )
 
+            def half_of(n):
+                r, half = divmod(n, HALVES)
+                return value[r][:, half * B_HALF : (half + 1) * B_HALF, :]
+
             def difference(n):
-                basis[n] = stage.tile([P, HALF_COLS], BF16, name="basis", align_bytes=64)
                 nc.vector.scalar_tensor_tensor(
-                    out=basis[n][:], in0=inner[n][:], scalar=0.0, in1=outer[n][:], op0=ALU.min, op1=ALU.subtract
+                    out=half_of(n), in0=inner[n][:], scalar=0.0, in1=outer[n][:], op0=ALU.min, op1=ALU.subtract
                 )
 
             def no_negatives(n):
-                nc.vector.tensor_scalar_max(out=basis[n][:], in0=basis[n][:], scalar1=0.0)
+                nc.vector.tensor_scalar_max(out=half_of(n), in0=half_of(n), scalar1=0.0)
 
-            def quantise_basis(n):
-                b_codes[n] = b_pool.tile([P, B_HALF], U32, name="b_codes", align_bytes=64)
-                b_scales[n] = b_pool.tile([P, B_HALF], U8, name="b_scales", align_bytes=64)
-                nc.vector.quantize_mx(out=b_codes[n][:].bitcast(FP8X4), scales=b_scales[n][:], in_=basis[n][:])
+            units = CLASSES * HALVES
 
-            def weight_views(g, first_j, last_j):
-                first = g * GROUP
-                count = min(GROUP, C - first)
-                if first_j == 0:
-                    grouped[g] = stage.tile([P, GROUP, J, PACK], BF16, name="grouped", align_bytes=64)
-                return (
-                    grouped[g][:, 0:count, first_j:last_j, :].rearrange("p c j t -> p j t c"),
-                    w_view[:, first_j:last_j, :, first : first + count],
+            with tc.tile_pool(name="setup", bufs=1, side="left") as setup:
+                warm = setup.tile([P, 1], F32)
+                nc.vector.memset(warm[:], 0.0)
+                nc.scalar.activation(out=warm[:], in_=warm[:], func=FUNC.Abs)
+                x_rows = setup.tile([P, B_TILES, I], BF16)
+                nc.sync.dma_start(out=x_rows[:], in_=x.rearrange("(m r) i -> r m i", r=P))
+                grid_bf = setup.tile([P, C], BF16)
+                nc.scalar.dma_start(out=grid_bf[:], in_=grid.partition_broadcast(P))
+                w_rows = spline_weight.rearrange("(p t) j c -> t p (j c)", t=PACK)
+                for t in range(PACK):
+                    nc.sync.dma_start(out=w_raw[:, t, :], in_=w_rows[t])
+                make_identity(nc, identity[:])
+                x_clip = setup.tile([P, B, PACK], BF16)
+                number = setup.tile([P, B_HALF, PACK], I32)
+
+                first.enter_context(tc.manual_schedule())
+                nc.vector.tensor_scalar(
+                    out=neg_grid[:], in0=grid_bf[:], scalar1=-1.0, scalar2=None, op0=ALU.mult
                 )
-
-            def quantise_weights(k):
-                w_codes[k] = stage.tile([P, J], U32, name="w_codes", align_bytes=64)
-                w_scales[k] = stage.tile([P, J], U8, name="w_scales", align_bytes=64)
-                nc.vector.quantize_mx(
-                    out=w_codes[k][:].bitcast(FP8X4),
-                    scales=w_scales[k][:],
-                    in_=grouped[k // GROUP][:, k % GROUP, :, :].rearrange("p j t -> p (j t)"),
+                nc.vector.tensor_tensor(
+                    out=steps[:, CLASSES:C],
+                    in0=grid_bf[:, 0 : C - CLASSES],
+                    in1=grid_bf[:, CLASSES:C],
+                    op=ALU.subtract,
                 )
-
-            def multiply(k):
                 for m in range(B_TILES):
-                    n = k * HALVES + m * P // B_HALF
-                    rows = slice(m * P % B_HALF, m * P % B_HALF + P)
-                    nc.tensor.matmul_mx(
-                        out=acc[m][:],
-                        lhsT=b_codes[n][:, rows].bitcast(FP8X4),
-                        lhsT_scale=b_scales[n][:, rows],
-                        rhs=w_codes[k][:].bitcast(FP8X4),
-                        rhs_scale=w_scales[k][:],
-                        start=(k == 0),
-                        stop=(k == C - 1),
+                    nc.vector.tensor_scalar(
+                        out=x_rows_clip[:, m, :, :],
+                        in0=x_rows[:, m, :].rearrange("r (p t) -> r t p", t=PACK),
+                        scalar1=0.99,
+                        scalar2=-0.99,
+                        op0=ALU.min,
+                        op1=ALU.max,
                     )
 
-            units = C * HALVES
-            distance(0)
-            for n in range(units + LAG * HALVES + 1):
-                g, step = divmod(n - LAG * HALVES, PIECES)
-                k = g * GROUP + step // HALVES
-                if n + 1 < units:
-                    distance(n + 1)
-                if n < units:
-                    squares(n)
-                if g == -1 and step >= PIECES - HALVES:
-                    half = step - (PIECES - HALVES)
-                    to_view, from_view = weight_views(0, half * (J // HALVES), (half + 1) * (J // HALVES))
-                    nc.vector.tensor_copy(out=to_view, in_=from_view)
-                ahead, piece = divmod(n - LAG * HALVES - LEAD, PIECES)
-                if ahead >= 0 and (ahead + 1) * GROUP < C:
-                    to_view, from_view = weight_views(ahead + 1, piece * J_PIECE, (piece + 1) * J_PIECE)
-                    if piece < SCALAR_PIECES:
-                        nc.scalar.copy(out=to_view, in_=from_view)
-                    else:
-                        nc.vector.tensor_copy(out=to_view, in_=from_view)
-                if n < units:
-                    cubes(n)
-                if 1 <= n <= units:
-                    no_negatives(n - 1)
-                if n < units:
-                    difference(n)
-                if 1 <= n <= units:
-                    quantise_basis(n - 1)
-                if 0 <= k < C and step % HALVES == 1:
-                    quantise_weights(k)
-                    multiply(k)
+                def clip_turned(m):
+                    nc.scalar.activation(
+                        out=x_clip[:, m * P : (m + 1) * P, :], in_=turn([x_rows_clip[:, m, :, :]]), func=FUNC.Copy
+                    )
 
-        with tc.tile_pool(name="result", bufs=B_TILES) as result:
+                def count(s, half):
+                    cols = slice(half * B_HALF, (half + 1) * B_HALF)
+                    nc.vector.tensor_scalar(
+                        out=number[:],
+                        in0=x_clip[:, cols, :],
+                        scalar1=1.0 / (CLASSES * H),
+                        scalar2=(1.0 / H - s * SHARE + 3) / CLASSES + 0.5,
+                        op0=ALU.mult,
+                        op1=ALU.add,
+                    )
+                    nc.scalar.activation(
+                        out=member[s][:, cols, :].rearrange("p b t -> p (b t)"),
+                        in_=number[:].rearrange("p b t -> p (b t)").bitcast(U32),
+                        func=FUNC.Copy,
+                    )
+
+                def unit_step(n):
+                    if n + 2 < units:
+                        moves(n + 2)
+                    if n + 1 < units:
+                        distance(n + 1)
+                        squares(n + 1)
+                    if n < units:
+                        cubes(n)
+                    if 1 <= n <= units:
+                        no_negatives(n - 1)
+                    if n < units:
+                        difference(n)
+
+                moves(0)
+                distance(0)
+                squares(0)
+                moves(1)
+                for n in range(EARLY * HALVES):
+                    unit_step(n)
+                    if n < B_TILES:
+                        clip_turned(n)
+                    else:
+                        count(n - B_TILES, 0)
+                        count(n - B_TILES, 1)
+
+            late = ctx.enter_context(tc.tile_pool(name="late", bufs=1, side="left"))
+            value.extend([late.tile([P, B, PACK], BF16, name="value%d" % r) for r in range(EARLY, CLASSES)])
+            for n in range(EARLY * HALVES, units + 1):
+                unit_step(n)
+
+        acc = [psum_acc.tile([P, J], F32, name="acc%d" % m) for m in range(B_TILES)]
+        w_view = w_raw[:].rearrange("p t (j c) -> p j t c", c=C)
+
+        with ExitStack() as second:
+            groups = second.enter_context(tc.tile_pool(name="groups", bufs=2, side="right"))
+            stage = second.enter_context(tc.tile_pool(name="stage", bufs=2, side="right"))
+            second.enter_context(tc.manual_schedule())
+
+            mask, basis, b_codes, b_scales, grouped, w_codes, w_scales = {}, {}, {}, {}, {}, {}, {}
+
+            def regroup(copy, g, piece):
+                first_c = g * GROUP
+                count_c = min(GROUP, C - first_c)
+                js = slice(piece * J_PIECE, (piece + 1) * J_PIECE)
+                if piece == 0:
+                    grouped[g] = groups.tile([P, GROUP, J, PACK], BF16, name="grouped", align_bytes=64)
+                copy(
+                    out=grouped[g][:, 0:count_c, js, :].rearrange("p c j t -> p j t c"),
+                    in_=w_view[:, js, :, first_c : first_c + count_c],
+                )
+
+            def make_mask(c):
+                r, k = c % CLASSES, c // CLASSES
+                s = r // SHARE
+                if r % SHARE == 0:
+                    mask[s, k] = stage.tile([P, B * PACK], BF16, name="mask", bufs=1)
+                    nc.vector.tensor_scalar(
+                        out=mask[s, k][:],
+                        in0=member[s][:].rearrange("p b t -> p (b t)"),
+                        scalar1=float(k + 1),
+                        scalar2=None,
+                        op0=ALU.is_equal,
+                    )
+
+            def expand(c):
+                r, k = c % CLASSES, c // CLASSES
+                basis[c] = stage.tile([P, B * PACK], BF16, name="basis", align_bytes=64)
+                nc.vector.tensor_tensor(
+                    out=basis[c][:],
+                    in0=value[r][:].rearrange("p b t -> p (b t)"),
+                    in1=mask[r // SHARE, k][:],
+                    op=ALU.mult,
+                )
+
+            def quantise_basis(c):
+                b_codes[c] = stage.tile([P, B], U32, name="b_codes", align_bytes=64)
+                b_scales[c] = stage.tile([P, B], U8, name="b_scales", align_bytes=64)
+                nc.vector.quantize_mx(out=b_codes[c][:].bitcast(FP8X4), scales=b_scales[c][:], in_=basis[c][:])
+
+            def quantise_weights(c):
+                w_codes[c] = stage.tile([P, J], U32, name="w_codes", align_bytes=64)
+                w_scales[c] = stage.tile([P, J], U8, name="w_scales", align_bytes=64)
+                nc.vector.quantize_mx(
+                    out=w_codes[c][:].bitcast(FP8X4),
+                    scales=w_scales[c][:],
+                    in_=grouped[c // GROUP][:, c % GROUP, :, :].rearrange("p j t -> p (j t)"),
+                )
+
+            def multiply(c):
+                for m in range(B_TILES):
+                    rows = slice(m * P, (m + 1) * P)
+                    nc.tensor.matmul_mx(
+                        out=acc[m][:],
+                        lhsT=b_codes[c][:, rows].bitcast(FP8X4),
+                        lhsT_scale=b_scales[c][:, rows],
+                        rhs=w_codes[c][:].bitcast(FP8X4),
+                        rhs_scale=w_scales[c][:],
+                        start=(c == 0),
+                        stop=(c == C - 1),
+                    )
+
+            for piece in range(PIECES):
+                regroup(nc.scalar.copy if piece < PIECES // 2 else nc.vector.tensor_copy, 0, piece)
+            for c in range(C + 1):
+                g, piece = divmod(c, GROUP)
+                if (g + 1) * GROUP < C:
+                    regroup(nc.scalar.copy, g + 1, piece)
+                if c < C:
+                    make_mask(c)
+                if c >= 1:
+                    quantise_weights(c - 1)
+                if c < C:
+                    expand(c)
+                if c >= 1:
+                    quantise_basis(c - 1)
+                    multiply(c - 1)
+
+        with tc.tile_pool(name="result", bufs=B_TILES, side="right") as result:
             for m in range(B_TILES):
                 out_rows = result.tile([P, J], F32)
                 if m % 2 == 0:

@@ -43,45 +43,48 @@ def tile_fastkanlayer_pa_kernel(tc, x, spline_weight, grid, out):
     nc = tc.nc
     with ExitStack() as ctx:
         keep = ctx.enter_context(tc.tile_pool(name="keep", bufs=1, side="left"))
-        psum_acc = ctx.enter_context(tc.psum_pool(name="psum_acc", bufs=1))
 
         w_raw = keep.tile([P, PACK, J * C], BF16)
         neg_grid = keep.tile([P, C], F32)
-        steps = keep.tile([P, C], F32)
+        sums = keep.tile([P, C], F32)
+        neg_sums = keep.tile([P, C], F32)
+        offset = keep.tile([P, CLASSES], F32)
         identity = keep.tile([P, P], F32)
         member = [keep.tile([P, B, PACK], BF16, name="member%d" % s) for s in range(SETS)]
         value = [keep.tile([P, B, PACK], BF16, name="value%d" % r) for r in range(EARLY)]
 
         with ExitStack() as first:
             wide = first.enter_context(tc.tile_pool(name="wide", bufs=1, side="right"))
-            step_pool = first.enter_context(tc.tile_pool(name="step_pool", bufs=10, side="right"))
+            hinge_pool = first.enter_context(tc.tile_pool(name="hinge_pool", bufs=10, side="right"))
             act = first.enter_context(tc.tile_pool(name="act", bufs=2, side="right"))
-            psum_u = first.enter_context(tc.psum_pool(name="psum_u", bufs=4))
+            psum_x = first.enter_context(tc.psum_pool(name="psum_x", bufs=8))
 
-            x_rows_clip = wide.tile([P, B_TILES, PACK, P], F32)
+            x_clip = wide.tile([P, PACK, B], F32)
 
-            pieces, dist, inner, outer = {}, {}, {}, {}
+            hinge, dist, inner, outer = {}, {}, {}, {}
 
-            def border(r, k):
-                return -1.0 + H * (CLASSES * k + r - r % SHARE - 3)
-
-            def moves(n):
+            def half_rows(n):
                 r, half = divmod(n, HALVES)
-                for m in range(half * M_HALF, (half + 1) * M_HALF):
+                return r, range(half * M_HALF, (half + 1) * M_HALF)
+
+            def hinges(n):
+                r, row_tiles = half_rows(n)
+                for m in row_tiles:
                     for k in range(1, MEMBERS):
                         c = r + CLASSES * k
-                        pieces[r, m, k] = step_pool.tile([P, PACK, P], F32, name="piece")
+                        odd = k % 2 == 1
+                        hinge[r, m, k] = hinge_pool.tile([P, PACK, P], F32, name="hinge")
                         nc.vector.tensor_scalar(
-                            out=pieces[r, m, k][:],
-                            in0=x_rows_clip[:, m, :, :],
-                            scalar1=border(r, k),
-                            scalar2=steps[:, c : c + 1],
-                            op0=ALU.is_ge,
-                            op1=ALU.mult,
+                            out=hinge[r, m, k][:],
+                            in0=x_clip[:, :, m * P : (m + 1) * P],
+                            scalar1=-2.0 if odd else 2.0,
+                            scalar2=(neg_sums if odd else sums)[:, c : c + 1],
+                            op0=ALU.mult,
+                            op1=ALU.min if odd else ALU.max,
                         )
 
-            def turn(parts):
-                turned = psum_u.tile([P, PACK, P], F32, name="turned")
+            def turned_sum(parts):
+                turned = psum_x.tile([P, PACK, P], F32, name="turned")
                 for t in range(PACK):
                     for i, part in enumerate(parts):
                         nc.tensor.matmul(
@@ -92,51 +95,49 @@ def tile_fastkanlayer_pa_kernel(tc, x, spline_weight, grid, out):
                             start=(i == 0),
                             stop=(i == len(parts) - 1),
                         )
-                return turned[:].rearrange("p t r -> p r t")
+                return turned
 
             def distance(n):
-                r, half = divmod(n, HALVES)
-                dist[n] = act.tile([P, B_HALF, PACK], F32, name="dist")
-                for m in range(M_HALF):
-                    mm = half * M_HALF + m
-                    signed = turn([x_rows_clip[:, mm, :, :]] + [pieces[r, mm, k] for k in range(1, MEMBERS)])
+                r, row_tiles = half_rows(n)
+                dist[n] = act.tile([P, M_HALF, PACK, P], F32, name="dist")
+                for i, m in enumerate(row_tiles):
+                    x_part = x_clip[:, :, m * P : (m + 1) * P]
+                    wave = turned_sum([x_part] + [hinge[r, m, k] for k in range(1, MEMBERS)])
                     nc.scalar.activation(
-                        out=dist[n][:, m * P : (m + 1) * P, :],
-                        in_=signed,
-                        func=FUNC.Abs,
-                        bias=neg_grid[:, r : r + 1],
-                        scale=1.0,
+                        out=dist[n][:, i, :, :], in_=wave[:], func=FUNC.Abs, bias=offset[:, r : r + 1], scale=1.0
                     )
 
             def squares(n):
-                outer[n] = act.tile([P, B_HALF, PACK], F32, name="outer")
-                nc.scalar.activation(
-                    out=outer[n][:], in_=dist[n][:], func=FUNC.Square, bias=OUTER_SCALE * REACH, scale=-OUTER_SCALE
-                )
-                inner[n] = act.tile([P, B_HALF, PACK], F32, name="inner")
+                inner[n] = act.tile([P, M_HALF, PACK, P], F32, name="inner")
                 nc.scalar.activation(
                     out=inner[n][:], in_=dist[n][:], func=FUNC.Square, bias=INNER_SCALE * H, scale=-INNER_SCALE
+                )
+                outer[n] = act.tile([P, M_HALF, PACK, P], F32, name="outer")
+                nc.scalar.activation(
+                    out=outer[n][:], in_=dist[n][:], func=FUNC.Square, bias=OUTER_SCALE * REACH, scale=-OUTER_SCALE
                 )
 
             def cubes(n):
                 nc.vector.scalar_tensor_tensor(
-                    out=outer[n][:], in0=dist[n][:], scalar=REACH, in1=outer[n][:], op0=ALU.subtract, op1=ALU.mult
-                )
-                nc.vector.scalar_tensor_tensor(
                     out=inner[n][:], in0=dist[n][:], scalar=H, in1=inner[n][:], op0=ALU.subtract, op1=ALU.mult
                 )
-
-            def half_of(n):
-                r, half = divmod(n, HALVES)
-                return value[r][:, half * B_HALF : (half + 1) * B_HALF, :]
-
-            def difference(n):
                 nc.vector.scalar_tensor_tensor(
-                    out=half_of(n), in0=inner[n][:], scalar=0.0, in1=outer[n][:], op0=ALU.min, op1=ALU.subtract
+                    out=outer[n][:], in0=dist[n][:], scalar=REACH, in1=outer[n][:], op0=ALU.subtract, op1=ALU.mult
+                )
+                nc.vector.tensor_scalar(
+                    out=inner[n][:], in0=inner[n][:], scalar1=-1.0, scalar2=0.0, op0=ALU.mult, op1=ALU.max
                 )
 
-            def no_negatives(n):
-                nc.vector.tensor_scalar_max(out=half_of(n), in0=half_of(n), scalar1=0.0)
+            def combine(n):
+                r, row_tiles = half_rows(n)
+                for i, m in enumerate(row_tiles):
+                    minus = turned_sum([outer[n][:, i, :, :], inner[n][:, i, :, :]])
+                    nc.scalar.activation(
+                        out=value[r][:, m * P : (m + 1) * P, :],
+                        in_=minus[:].rearrange("p t b -> p b t"),
+                        func=FUNC.Relu,
+                        scale=-1.0,
+                    )
 
             units = CLASSES * HALVES
 
@@ -152,7 +153,6 @@ def tile_fastkanlayer_pa_kernel(tc, x, spline_weight, grid, out):
                 for t in range(PACK):
                     nc.sync.dma_start(out=w_raw[:, t, :], in_=w_rows[t])
                 make_identity(nc, identity[:])
-                x_clip = setup.tile([P, B, PACK], BF16)
                 number = setup.tile([P, B_HALF, PACK], I32)
 
                 first.enter_context(tc.manual_schedule())
@@ -160,72 +160,85 @@ def tile_fastkanlayer_pa_kernel(tc, x, spline_weight, grid, out):
                     out=neg_grid[:], in0=grid_bf[:], scalar1=-1.0, scalar2=None, op0=ALU.mult
                 )
                 nc.vector.tensor_tensor(
-                    out=steps[:, CLASSES:C],
-                    in0=grid_bf[:, 0 : C - CLASSES],
-                    in1=grid_bf[:, CLASSES:C],
-                    op=ALU.subtract,
+                    out=sums[:, CLASSES:C], in0=grid_bf[:, 0 : C - CLASSES], in1=grid_bf[:, CLASSES:C], op=ALU.add
                 )
-                for m in range(B_TILES):
+                nc.vector.tensor_scalar(
+                    out=neg_sums[:, CLASSES:C], in0=sums[:, CLASSES:C], scalar1=-1.0, scalar2=None, op0=ALU.mult
+                )
+                before = neg_grid[:, 0:CLASSES]
+                for k in range(1, MEMBERS):
+                    nc.vector.tensor_tensor(
+                        out=offset[:],
+                        in0=before,
+                        in1=sums[:, k * CLASSES : (k + 1) * CLASSES],
+                        op=ALU.add if k % 2 == 1 else ALU.subtract,
+                    )
+                    before = offset[:]
+
+                for half in range(HALVES):
+                    pairs = psum_x.tile([P, 2, B_HALF], F32, name="turned")
+                    for m in range(M_HALF):
+                        words = x_rows[:, half * M_HALF + m, :].bitcast(F32)
+                        words = words.rearrange("r (p u) -> r u p", u=2)
+                        for u in range(2):
+                            nc.tensor.transpose(
+                                out=pairs[:, u, m * P : (m + 1) * P], in_=words[:, u, :], identity=identity[:]
+                            )
                     nc.vector.tensor_scalar(
-                        out=x_rows_clip[:, m, :, :],
-                        in0=x_rows[:, m, :].rearrange("r (p t) -> r t p", t=PACK),
+                        out=x_clip[:, :, half * B_HALF : (half + 1) * B_HALF].rearrange(
+                            "p (u e) b -> p u e b", e=2
+                        ),
+                        in0=pairs[:]
+                        .rearrange("p u b -> p (u b)")
+                        .bitcast(BF16)
+                        .rearrange("p (u b e) -> p u e b", u=2, e=2),
                         scalar1=0.99,
                         scalar2=-0.99,
                         op0=ALU.min,
                         op1=ALU.max,
                     )
 
-                def clip_turned(m):
-                    nc.scalar.activation(
-                        out=x_clip[:, m * P : (m + 1) * P, :], in_=turn([x_rows_clip[:, m, :, :]]), func=FUNC.Copy
-                    )
-
                 def count(s, half):
-                    cols = slice(half * B_HALF, (half + 1) * B_HALF)
+                    rows = slice(half * B_HALF, (half + 1) * B_HALF)
                     nc.vector.tensor_scalar(
                         out=number[:],
-                        in0=x_clip[:, cols, :],
+                        in0=x_clip[:, :, rows].rearrange("p t b -> p b t"),
                         scalar1=1.0 / (CLASSES * H),
                         scalar2=(1.0 / H - s * SHARE + 3) / CLASSES + 0.5,
                         op0=ALU.mult,
                         op1=ALU.add,
                     )
                     nc.scalar.activation(
-                        out=member[s][:, cols, :].rearrange("p b t -> p (b t)"),
+                        out=member[s][:, rows, :].rearrange("p b t -> p (b t)"),
                         in_=number[:].rearrange("p b t -> p (b t)").bitcast(U32),
                         func=FUNC.Copy,
                     )
 
                 def unit_step(n):
+                    if 1 <= n <= units:
+                        combine(n - 1)
                     if n + 2 < units:
-                        moves(n + 2)
+                        hinges(n + 2)
                     if n + 1 < units:
                         distance(n + 1)
                         squares(n + 1)
                     if n < units:
                         cubes(n)
-                    if 1 <= n <= units:
-                        no_negatives(n - 1)
-                    if n < units:
-                        difference(n)
 
-                moves(0)
+                hinges(0)
                 distance(0)
                 squares(0)
-                moves(1)
+                hinges(1)
                 for n in range(EARLY * HALVES):
                     unit_step(n)
-                    if n < B_TILES:
-                        clip_turned(n)
-                    else:
-                        count(n - B_TILES, 0)
-                        count(n - B_TILES, 1)
+                    count(n // HALVES, n % HALVES)
 
             late = ctx.enter_context(tc.tile_pool(name="late", bufs=1, side="left"))
             value.extend([late.tile([P, B, PACK], BF16, name="value%d" % r) for r in range(EARLY, CLASSES)])
             for n in range(EARLY * HALVES, units + 1):
                 unit_step(n)
 
+        psum_acc = ctx.enter_context(tc.psum_pool(name="psum_acc", bufs=1))
         acc = [psum_acc.tile([P, J], F32, name="acc%d" % m) for m in range(B_TILES)]
         w_view = w_raw[:].rearrange("p t (j c) -> p j t c", c=C)
 

@@ -20,7 +20,6 @@ B_TILES = B // P
 HALVES = 2
 B_HALF = B // HALVES
 M_HALF = B_HALF // P
-HALF_COLS = B_HALF * PACK
 FLOPS = 2 * B * J * C * I
 
 H = 2.0 / (C - 1)
@@ -55,33 +54,28 @@ def tile_fastkanlayer_pa_kernel(tc, x, spline_weight, grid, out):
 
         with ExitStack() as first:
             wide = first.enter_context(tc.tile_pool(name="wide", bufs=1, side="right"))
-            hinge_pool = first.enter_context(tc.tile_pool(name="hinge_pool", bufs=10, side="right"))
-            act = first.enter_context(tc.tile_pool(name="act", bufs=2, side="right"))
+            hinge_pool = first.enter_context(tc.tile_pool(name="hinge_pool", bufs=12, side="right"))
+            act = first.enter_context(tc.tile_pool(name="act", bufs=3, side="right"))
             psum_x = first.enter_context(tc.psum_pool(name="psum_x", bufs=8))
 
             x_clip = wide.tile([P, PACK, B], F32)
 
             hinge, dist, inner, outer = {}, {}, {}, {}
 
-            def half_rows(n):
-                r, half = divmod(n, HALVES)
-                return r, range(half * M_HALF, (half + 1) * M_HALF)
-
             def hinges(n):
-                r, row_tiles = half_rows(n)
-                for m in row_tiles:
-                    for k in range(1, MEMBERS):
-                        c = r + CLASSES * k
-                        odd = k % 2 == 1
-                        hinge[r, m, k] = hinge_pool.tile([P, PACK, P], F32, name="hinge")
-                        nc.vector.tensor_scalar(
-                            out=hinge[r, m, k][:],
-                            in0=x_clip[:, :, m * P : (m + 1) * P],
-                            scalar1=-2.0 if odd else 2.0,
-                            scalar2=(neg_sums if odd else sums)[:, c : c + 1],
-                            op0=ALU.mult,
-                            op1=ALU.min if odd else ALU.max,
-                        )
+                r, m = divmod(n, B_TILES)
+                for k in range(1, MEMBERS):
+                    c = r + CLASSES * k
+                    odd = k % 2 == 1
+                    hinge[n, k] = hinge_pool.tile([P, PACK, P], F32, name="hinge")
+                    nc.vector.tensor_scalar(
+                        out=hinge[n, k][:],
+                        in0=x_clip[:, :, m * P : (m + 1) * P],
+                        scalar1=-2.0 if odd else 2.0,
+                        scalar2=(neg_sums if odd else sums)[:, c : c + 1],
+                        op0=ALU.mult,
+                        op1=ALU.min if odd else ALU.max,
+                    )
 
             def turned_sum(parts):
                 turned = psum_x.tile([P, PACK, P], F32, name="turned")
@@ -98,21 +92,20 @@ def tile_fastkanlayer_pa_kernel(tc, x, spline_weight, grid, out):
                 return turned
 
             def distance(n):
-                r, row_tiles = half_rows(n)
-                dist[n] = act.tile([P, M_HALF, PACK, P], F32, name="dist")
-                for i, m in enumerate(row_tiles):
-                    x_part = x_clip[:, :, m * P : (m + 1) * P]
-                    wave = turned_sum([x_part] + [hinge[r, m, k] for k in range(1, MEMBERS)])
-                    nc.scalar.activation(
-                        out=dist[n][:, i, :, :], in_=wave[:], func=FUNC.Abs, bias=offset[:, r : r + 1], scale=1.0
-                    )
+                r, m = divmod(n, B_TILES)
+                dist[n] = act.tile([P, PACK, P], F32, name="dist", bufs=4)
+                x_part = x_clip[:, :, m * P : (m + 1) * P]
+                wave = turned_sum([x_part] + [hinge[n, k] for k in range(1, MEMBERS)])
+                nc.scalar.activation(
+                    out=dist[n][:], in_=wave[:], func=FUNC.Abs, bias=offset[:, r : r + 1], scale=1.0
+                )
 
             def squares(n):
-                inner[n] = act.tile([P, M_HALF, PACK, P], F32, name="inner")
+                inner[n] = act.tile([P, PACK, P], F32, name="inner")
                 nc.scalar.activation(
                     out=inner[n][:], in_=dist[n][:], func=FUNC.Square, bias=INNER_SCALE * H, scale=-INNER_SCALE
                 )
-                outer[n] = act.tile([P, M_HALF, PACK, P], F32, name="outer")
+                outer[n] = act.tile([P, PACK, P], F32, name="outer")
                 nc.scalar.activation(
                     out=outer[n][:], in_=dist[n][:], func=FUNC.Square, bias=OUTER_SCALE * REACH, scale=-OUTER_SCALE
                 )
@@ -129,17 +122,16 @@ def tile_fastkanlayer_pa_kernel(tc, x, spline_weight, grid, out):
                 )
 
             def combine(n):
-                r, row_tiles = half_rows(n)
-                for i, m in enumerate(row_tiles):
-                    minus = turned_sum([outer[n][:, i, :, :], inner[n][:, i, :, :]])
-                    nc.scalar.activation(
-                        out=value[r][:, m * P : (m + 1) * P, :],
-                        in_=minus[:].rearrange("p t b -> p b t"),
-                        func=FUNC.Relu,
-                        scale=-1.0,
-                    )
+                r, m = divmod(n, B_TILES)
+                minus = turned_sum([outer[n], inner[n]])
+                nc.scalar.activation(
+                    out=value[r][:, m * P : (m + 1) * P, :],
+                    in_=minus[:].rearrange("p t b -> p b t"),
+                    func=FUNC.Relu,
+                    scale=-1.0,
+                )
 
-            units = CLASSES * HALVES
+            units = CLASSES * B_TILES
 
             with tc.tile_pool(name="setup", bufs=1, side="left") as setup:
                 warm = setup.tile([P, 1], F32)
@@ -215,27 +207,25 @@ def tile_fastkanlayer_pa_kernel(tc, x, spline_weight, grid, out):
                     )
 
                 def unit_step(n):
-                    if 1 <= n <= units:
-                        combine(n - 1)
-                    if n + 2 < units:
-                        hinges(n + 2)
-                    if n + 1 < units:
-                        distance(n + 1)
+                    if 0 <= n + 3 < units:
+                        hinges(n + 3)
+                    if 0 <= n + 2 < units:
+                        distance(n + 2)
+                    if 0 <= n + 1 < units:
                         squares(n + 1)
-                    if n < units:
+                    if 0 <= n < units:
                         cubes(n)
+                    if 0 <= n - 1 < units:
+                        combine(n - 1)
 
-                hinges(0)
-                distance(0)
-                squares(0)
-                hinges(1)
-                for n in range(EARLY * HALVES):
+                for n in range(-3, EARLY * B_TILES):
                     unit_step(n)
-                    count(n // HALVES, n % HALVES)
+                    if n >= 0 and n % 2 == 0:
+                        count(n // 4, n // 2 % 2)
 
             late = ctx.enter_context(tc.tile_pool(name="late", bufs=1, side="left"))
             value.extend([late.tile([P, B, PACK], BF16, name="value%d" % r) for r in range(EARLY, CLASSES)])
-            for n in range(EARLY * HALVES, units + 1):
+            for n in range(EARLY * B_TILES, units + 1):
                 unit_step(n)
 
         psum_acc = ctx.enter_context(tc.psum_pool(name="psum_acc", bufs=1))

@@ -33,9 +33,10 @@ SHARE = 2
 SETS = -(-CLASSES // SHARE)
 EARLY = 4
 
-GROUP = 4
+GROUP = 3
 PIECES = 4
 J_PIECE = J // PIECES
+LAG = 3
 
 
 def tile_fastkanlayer_pa_kernel(tc, x, spline_weight, grid, out):
@@ -46,7 +47,7 @@ def tile_fastkanlayer_pa_kernel(tc, x, spline_weight, grid, out):
         w_raw = keep.tile([P, PACK, J * C], BF16)
         neg_grid = keep.tile([P, C], F32)
         sums = keep.tile([P, C], F32)
-        neg_sums = keep.tile([P, C], F32)
+        mids = keep.tile([P, C], F32)
         offset = keep.tile([P, CLASSES], F32)
         identity = keep.tile([P, P], F32)
         member = [keep.tile([P, B, PACK], BF16, name="member%d" % s) for s in range(SETS)]
@@ -54,27 +55,27 @@ def tile_fastkanlayer_pa_kernel(tc, x, spline_weight, grid, out):
 
         with ExitStack() as first:
             wide = first.enter_context(tc.tile_pool(name="wide", bufs=1, side="right"))
-            hinge_pool = first.enter_context(tc.tile_pool(name="hinge_pool", bufs=12, side="right"))
+            clamp_pool = first.enter_context(tc.tile_pool(name="clamp_pool", bufs=8, side="right"))
             act = first.enter_context(tc.tile_pool(name="act", bufs=3, side="right"))
             psum_x = first.enter_context(tc.psum_pool(name="psum_x", bufs=8))
 
             x_clip = wide.tile([P, PACK, B], F32)
+            x_part = wide.tile([P, PACK, B], F32)
 
-            hinge, dist, inner, outer = {}, {}, {}, {}
+            clamp, dist, inner, outer = {}, {}, {}, {}
 
-            def hinges(n):
+            def clamps(n):
                 r, m = divmod(n, B_TILES)
-                for k in range(1, MEMBERS):
+                for k in range(1, MEMBERS, 2):
                     c = r + CLASSES * k
-                    odd = k % 2 == 1
-                    hinge[n, k] = hinge_pool.tile([P, PACK, P], F32, name="hinge")
+                    clamp[n, k] = clamp_pool.tile([P, PACK, P], F32, name="clamp")
                     nc.vector.tensor_scalar(
-                        out=hinge[n, k][:],
+                        out=clamp[n, k][:],
                         in0=x_clip[:, :, m * P : (m + 1) * P],
-                        scalar1=-2.0 if odd else 2.0,
-                        scalar2=(neg_sums if odd else sums)[:, c : c + 1],
-                        op0=ALU.mult,
-                        op1=ALU.min if odd else ALU.max,
+                        scalar1=mids[:, c : c + 1],
+                        scalar2=mids[:, c + CLASSES : c + CLASSES + 1],
+                        op0=ALU.max,
+                        op1=ALU.min,
                     )
 
             def turned_sum(parts):
@@ -94,10 +95,9 @@ def tile_fastkanlayer_pa_kernel(tc, x, spline_weight, grid, out):
             def distance(n):
                 r, m = divmod(n, B_TILES)
                 dist[n] = act.tile([P, PACK, P], F32, name="dist", bufs=4)
-                x_part = x_clip[:, :, m * P : (m + 1) * P]
-                wave = turned_sum([x_part] + [hinge[n, k] for k in range(1, MEMBERS)])
+                wave = turned_sum([x_part[:, :, m * P : (m + 1) * P]] + [clamp[n, k] for k in range(1, MEMBERS, 2)])
                 nc.scalar.activation(
-                    out=dist[n][:], in_=wave[:], func=FUNC.Abs, bias=offset[:, r : r + 1], scale=1.0
+                    out=dist[n][:], in_=wave[:], func=FUNC.Abs, bias=offset[:, r : r + 1], scale=-2.0
                 )
 
             def squares(n):
@@ -155,15 +155,12 @@ def tile_fastkanlayer_pa_kernel(tc, x, spline_weight, grid, out):
                     out=sums[:, CLASSES:C], in0=grid_bf[:, 0 : C - CLASSES], in1=grid_bf[:, CLASSES:C], op=ALU.add
                 )
                 nc.vector.tensor_scalar(
-                    out=neg_sums[:, CLASSES:C], in0=sums[:, CLASSES:C], scalar1=-1.0, scalar2=None, op0=ALU.mult
+                    out=mids[:, CLASSES:C], in0=sums[:, CLASSES:C], scalar1=0.5, scalar2=None, op0=ALU.mult
                 )
                 before = neg_grid[:, 0:CLASSES]
-                for k in range(1, MEMBERS):
+                for k in range(1, MEMBERS, 2):
                     nc.vector.tensor_tensor(
-                        out=offset[:],
-                        in0=before,
-                        in1=sums[:, k * CLASSES : (k + 1) * CLASSES],
-                        op=ALU.add if k % 2 == 1 else ALU.subtract,
+                        out=offset[:], in0=before, in1=sums[:, k * CLASSES : (k + 1) * CLASSES], op=ALU.add
                     )
                     before = offset[:]
 
@@ -189,6 +186,12 @@ def tile_fastkanlayer_pa_kernel(tc, x, spline_weight, grid, out):
                         op0=ALU.min,
                         op1=ALU.max,
                     )
+                    nc.scalar.activation(
+                        out=x_part[:, :, half * B_HALF : (half + 1) * B_HALF],
+                        in_=x_clip[:, :, half * B_HALF : (half + 1) * B_HALF],
+                        func=FUNC.Copy,
+                        scale=-0.5,
+                    )
 
                 def count(s, half):
                     rows = slice(half * B_HALF, (half + 1) * B_HALF)
@@ -200,15 +203,14 @@ def tile_fastkanlayer_pa_kernel(tc, x, spline_weight, grid, out):
                         op0=ALU.mult,
                         op1=ALU.add,
                     )
-                    nc.scalar.activation(
-                        out=member[s][:, rows, :].rearrange("p b t -> p (b t)"),
-                        in_=number[:].rearrange("p b t -> p (b t)").bitcast(U32),
-                        func=FUNC.Copy,
-                    )
+
+                def to_member(s, half):
+                    rows = slice(half * B_HALF, (half + 1) * B_HALF)
+                    nc.vector.tensor_copy(out=member[s][:, rows, :], in_=number[:])
 
                 def unit_step(n):
                     if 0 <= n + 3 < units:
-                        hinges(n + 3)
+                        clamps(n + 3)
                     if 0 <= n + 2 < units:
                         distance(n + 2)
                     if 0 <= n + 1 < units:
@@ -220,8 +222,8 @@ def tile_fastkanlayer_pa_kernel(tc, x, spline_weight, grid, out):
 
                 for n in range(-3, EARLY * B_TILES):
                     unit_step(n)
-                    if n >= 0 and n % 2 == 0:
-                        count(n // 4, n // 2 % 2)
+                    if n >= 0:
+                        (count if n % 2 == 0 else to_member)(n // 4, n // 2 % 2)
 
             late = ctx.enter_context(tc.tile_pool(name="late", bufs=1, side="left"))
             value.extend([late.tile([P, B, PACK], BF16, name="value%d" % r) for r in range(EARLY, CLASSES)])
@@ -239,16 +241,16 @@ def tile_fastkanlayer_pa_kernel(tc, x, spline_weight, grid, out):
 
             mask, basis, b_codes, b_scales, grouped, w_codes, w_scales = {}, {}, {}, {}, {}, {}, {}
 
-            def regroup(copy, g, piece):
+            def regroup(g):
                 first_c = g * GROUP
                 count_c = min(GROUP, C - first_c)
-                js = slice(piece * J_PIECE, (piece + 1) * J_PIECE)
-                if piece == 0:
-                    grouped[g] = groups.tile([P, GROUP, J, PACK], BF16, name="grouped", align_bytes=64)
-                copy(
-                    out=grouped[g][:, 0:count_c, js, :].rearrange("p c j t -> p j t c"),
-                    in_=w_view[:, js, :, first_c : first_c + count_c],
-                )
+                grouped[g] = groups.tile([P, GROUP, J, PACK], BF16, name="grouped", align_bytes=64)
+                for piece in range(PIECES):
+                    js = slice(piece * J_PIECE, (piece + 1) * J_PIECE)
+                    nc.scalar.copy(
+                        out=grouped[g][:, 0:count_c, js, :].rearrange("p c j t -> p j t c"),
+                        in_=w_view[:, js, :, first_c : first_c + count_c],
+                    )
 
             def make_mask(c):
                 r, k = c % CLASSES, c // CLASSES
@@ -274,8 +276,8 @@ def tile_fastkanlayer_pa_kernel(tc, x, spline_weight, grid, out):
                 )
 
             def quantise_basis(c):
-                b_codes[c] = stage.tile([P, B], U32, name="b_codes", align_bytes=64)
-                b_scales[c] = stage.tile([P, B], U8, name="b_scales", align_bytes=64)
+                b_codes[c] = stage.tile([P, B], U32, name="b_codes", bufs=LAG + 1, align_bytes=64)
+                b_scales[c] = stage.tile([P, B], U8, name="b_scales", bufs=LAG + 1, align_bytes=64)
                 nc.vector.quantize_mx(out=b_codes[c][:].bitcast(FP8X4), scales=b_scales[c][:], in_=basis[c][:])
 
             def quantise_weights(c):
@@ -300,21 +302,21 @@ def tile_fastkanlayer_pa_kernel(tc, x, spline_weight, grid, out):
                         stop=(c == C - 1),
                     )
 
-            for piece in range(PIECES):
-                regroup(nc.scalar.copy if piece < PIECES // 2 else nc.vector.tensor_copy, 0, piece)
-            for c in range(C + 1):
-                g, piece = divmod(c, GROUP)
-                if (g + 1) * GROUP < C:
-                    regroup(nc.scalar.copy, g + 1, piece)
+            regroup(0)
+            for c in range(C + LAG):
+                w = c - LAG
+                if w >= 0 and w % GROUP == 0 and (w // GROUP + 1) * GROUP < C:
+                    regroup(w // GROUP + 1)
                 if c < C:
                     make_mask(c)
-                if c >= 1:
-                    quantise_weights(c - 1)
+                if w >= 0:
+                    quantise_weights(w)
                 if c < C:
                     expand(c)
-                if c >= 1:
+                if 1 <= c <= C:
                     quantise_basis(c - 1)
-                    multiply(c - 1)
+                if w >= 0:
+                    multiply(w)
 
         with tc.tile_pool(name="result", bufs=B_TILES, side="right") as result:
             for m in range(B_TILES):

@@ -17,9 +17,6 @@ P = 128
 PACK = 4
 B, I, J, C = 512, 512, 512, 35
 B_TILES = B // P
-HALVES = 2
-B_HALF = B // HALVES
-M_HALF = B_HALF // P
 FLOPS = 2 * B * J * C * I
 
 H = 2.0 / (C - 1)
@@ -34,6 +31,7 @@ SETS = -(-CLASSES // SHARE)
 EARLY = 4
 
 GROUP = 3
+STARTS = [0] + list(range(2, C, GROUP))
 PIECES = 4
 J_PIECE = J // PIECES
 LAG = 3
@@ -61,6 +59,7 @@ def tile_fastkanlayer_pa_kernel(tc, x, spline_weight, grid, out):
 
             x_clip = wide.tile([P, PACK, B], F32)
             x_part = wide.tile([P, PACK, B], F32)
+            number = wide.tile([P, P, PACK], I32)
 
             clamp, dist, inner, outer = {}, {}, {}, {}
 
@@ -138,14 +137,13 @@ def tile_fastkanlayer_pa_kernel(tc, x, spline_weight, grid, out):
                 nc.vector.memset(warm[:], 0.0)
                 nc.scalar.activation(out=warm[:], in_=warm[:], func=FUNC.Abs)
                 x_rows = setup.tile([P, B_TILES, I], BF16)
-                nc.sync.dma_start(out=x_rows[:], in_=x.rearrange("(m r) i -> r m i", r=P))
                 grid_bf = setup.tile([P, C], BF16)
-                nc.scalar.dma_start(out=grid_bf[:], in_=grid.partition_broadcast(P))
+                nc.sync.dma_start(out=grid_bf[:], in_=grid.partition_broadcast(P))
+                nc.sync.dma_start(out=x_rows[:], in_=x.rearrange("(m r) i -> r m i", r=P))
                 w_rows = spline_weight.rearrange("(p t) j c -> t p (j c)", t=PACK)
                 for t in range(PACK):
                     nc.sync.dma_start(out=w_raw[:, t, :], in_=w_rows[t])
                 make_identity(nc, identity[:])
-                number = setup.tile([P, B_HALF, PACK], I32)
 
                 first.enter_context(tc.manual_schedule())
                 nc.vector.tensor_scalar(
@@ -164,19 +162,14 @@ def tile_fastkanlayer_pa_kernel(tc, x, spline_weight, grid, out):
                     )
                     before = offset[:]
 
-                for half in range(HALVES):
-                    pairs = psum_x.tile([P, 2, B_HALF], F32, name="turned")
-                    for m in range(M_HALF):
-                        words = x_rows[:, half * M_HALF + m, :].bitcast(F32)
-                        words = words.rearrange("r (p u) -> r u p", u=2)
-                        for u in range(2):
-                            nc.tensor.transpose(
-                                out=pairs[:, u, m * P : (m + 1) * P], in_=words[:, u, :], identity=identity[:]
-                            )
+                def load_x(m):
+                    rows = slice(m * P, (m + 1) * P)
+                    pairs = psum_x.tile([P, 2, P], F32, name="turned")
+                    words = x_rows[:, m, :].bitcast(F32).rearrange("r (p u) -> r u p", u=2)
+                    for u in range(2):
+                        nc.tensor.transpose(out=pairs[:, u, :], in_=words[:, u, :], identity=identity[:])
                     nc.vector.tensor_scalar(
-                        out=x_clip[:, :, half * B_HALF : (half + 1) * B_HALF].rearrange(
-                            "p (u e) b -> p u e b", e=2
-                        ),
+                        out=x_clip[:, :, rows].rearrange("p (u e) b -> p u e b", e=2),
                         in0=pairs[:]
                         .rearrange("p u b -> p (u b)")
                         .bitcast(BF16)
@@ -187,28 +180,27 @@ def tile_fastkanlayer_pa_kernel(tc, x, spline_weight, grid, out):
                         op1=ALU.max,
                     )
                     nc.scalar.activation(
-                        out=x_part[:, :, half * B_HALF : (half + 1) * B_HALF],
-                        in_=x_clip[:, :, half * B_HALF : (half + 1) * B_HALF],
-                        func=FUNC.Copy,
-                        scale=-0.5,
+                        out=x_part[:, :, rows], in_=x_clip[:, :, rows], func=FUNC.Copy, scale=-0.5
                     )
 
-                def count(s, half):
-                    rows = slice(half * B_HALF, (half + 1) * B_HALF)
+                def count(s, m):
                     nc.vector.tensor_scalar(
                         out=number[:],
-                        in0=x_clip[:, :, rows].rearrange("p t b -> p b t"),
+                        in0=x_clip[:, :, m * P : (m + 1) * P].rearrange("p t b -> p b t"),
                         scalar1=1.0 / (CLASSES * H),
                         scalar2=(1.0 / H - s * SHARE + 3) / CLASSES + 0.5,
                         op0=ALU.mult,
                         op1=ALU.add,
                     )
 
-                def to_member(s, half):
-                    rows = slice(half * B_HALF, (half + 1) * B_HALF)
-                    nc.vector.tensor_copy(out=member[s][:, rows, :], in_=number[:])
+                def to_member(s, m):
+                    nc.vector.tensor_copy(out=member[s][:, m * P : (m + 1) * P, :], in_=number[:])
+
+                counting = [(f, s, m) for s in range(SETS) for m in range(B_TILES) for f in (count, to_member)]
 
                 def unit_step(n):
+                    if 0 <= n + 3 < B_TILES:
+                        load_x(n + 3)
                     if 0 <= n + 3 < units:
                         clamps(n + 3)
                     if 0 <= n + 2 < units:
@@ -217,13 +209,14 @@ def tile_fastkanlayer_pa_kernel(tc, x, spline_weight, grid, out):
                         squares(n + 1)
                     if 0 <= n < units:
                         cubes(n)
+                        share = len(counting)
+                        for f, s, m in counting[n * share // units : (n + 1) * share // units]:
+                            f(s, m)
                     if 0 <= n - 1 < units:
                         combine(n - 1)
 
                 for n in range(-3, EARLY * B_TILES):
                     unit_step(n)
-                    if n >= 0:
-                        (count if n % 2 == 0 else to_member)(n // 4, n // 2 % 2)
 
             late = ctx.enter_context(tc.tile_pool(name="late", bufs=1, side="left"))
             value.extend([late.tile([P, B, PACK], BF16, name="value%d" % r) for r in range(EARLY, CLASSES)])
@@ -239,11 +232,13 @@ def tile_fastkanlayer_pa_kernel(tc, x, spline_weight, grid, out):
             stage = second.enter_context(tc.tile_pool(name="stage", bufs=2, side="right"))
             second.enter_context(tc.manual_schedule())
 
-            mask, basis, b_codes, b_scales, grouped, w_codes, w_scales = {}, {}, {}, {}, {}, {}, {}
+            mask, basis, b_codes, b_scales, grouped, w_codes, w_scales, place = {}, {}, {}, {}, {}, {}, {}, {}
 
             def regroup(g):
-                first_c = g * GROUP
-                count_c = min(GROUP, C - first_c)
+                first_c = STARTS[g]
+                count_c = (STARTS + [C])[g + 1] - first_c
+                for c in range(first_c, first_c + count_c):
+                    place[c] = (g, c - first_c)
                 grouped[g] = groups.tile([P, GROUP, J, PACK], BF16, name="grouped", align_bytes=64)
                 for piece in range(PIECES):
                     js = slice(piece * J_PIECE, (piece + 1) * J_PIECE)
@@ -286,7 +281,7 @@ def tile_fastkanlayer_pa_kernel(tc, x, spline_weight, grid, out):
                 nc.vector.quantize_mx(
                     out=w_codes[c][:].bitcast(FP8X4),
                     scales=w_scales[c][:],
-                    in_=grouped[c // GROUP][:, c % GROUP, :, :].rearrange("p j t -> p (j t)"),
+                    in_=grouped[place[c][0]][:, place[c][1], :, :].rearrange("p j t -> p (j t)"),
                 )
 
             def multiply(c):
@@ -305,8 +300,8 @@ def tile_fastkanlayer_pa_kernel(tc, x, spline_weight, grid, out):
             regroup(0)
             for c in range(C + LAG):
                 w = c - LAG
-                if w >= 0 and w % GROUP == 0 and (w // GROUP + 1) * GROUP < C:
-                    regroup(w // GROUP + 1)
+                if w in STARTS[:-1]:
+                    regroup(STARTS.index(w) + 1)
                 if c < C:
                     make_mask(c)
                 if w >= 0:

@@ -77,7 +77,7 @@ def tile_fastkanlayer_pa_kernel(tc, x, spline_weight, grid, out):
                         op1=ALU.min,
                     )
 
-            def turned_sum(parts):
+            def turned_sum(parts, multiplied=()):
                 turned = psum_x.tile([P, PACK, P], F32, name="turned")
                 for t in range(PACK):
                     for i, part in enumerate(parts):
@@ -85,7 +85,7 @@ def tile_fastkanlayer_pa_kernel(tc, x, spline_weight, grid, out):
                             out=turned[:, t, :],
                             lhsT=part[:, t, :],
                             rhs=identity[:],
-                            is_transpose=True,
+                            is_transpose=(i > 0 or t not in multiplied),
                             start=(i == 0),
                             stop=(i == len(parts) - 1),
                         )
@@ -94,7 +94,10 @@ def tile_fastkanlayer_pa_kernel(tc, x, spline_weight, grid, out):
             def distance(n):
                 r, m = divmod(n, B_TILES)
                 dist[n] = act.tile([P, PACK, P], F32, name="dist", bufs=4)
-                wave = turned_sum([x_part[:, :, m * P : (m + 1) * P]] + [clamp[n, k] for k in range(1, MEMBERS, 2)])
+                wave = turned_sum(
+                    [x_part[:, :, m * P : (m + 1) * P]] + [clamp[n, k] for k in range(1, MEMBERS, 2)],
+                    multiplied=range(0, PACK, 2),
+                )
                 nc.scalar.activation(
                     out=dist[n][:], in_=wave[:], func=FUNC.Abs, bias=offset[:, r : r + 1], scale=-2.0
                 )
@@ -137,9 +140,9 @@ def tile_fastkanlayer_pa_kernel(tc, x, spline_weight, grid, out):
                 nc.vector.memset(warm[:], 0.0)
                 nc.scalar.activation(out=warm[:], in_=warm[:], func=FUNC.Abs)
                 x_rows = setup.tile([P, B_TILES, I], BF16)
+                nc.sync.dma_start(out=x_rows[:], in_=x.rearrange("(m r) i -> r m i", r=P))
                 grid_bf = setup.tile([P, C], BF16)
                 nc.sync.dma_start(out=grid_bf[:], in_=grid.partition_broadcast(P))
-                nc.sync.dma_start(out=x_rows[:], in_=x.rearrange("(m r) i -> r m i", r=P))
                 w_rows = spline_weight.rearrange("(p t) j c -> t p (j c)", t=PACK)
                 for t in range(PACK):
                     nc.sync.dma_start(out=w_raw[:, t, :], in_=w_rows[t])

@@ -34,7 +34,7 @@ GROUP = 3
 STARTS = [0] + list(range(2, C, GROUP))
 PIECES = 4
 J_PIECE = J // PIECES
-LAG = 3
+LAG = 4
 
 
 def tile_fastkanlayer_pa_kernel(tc, x, spline_weight, grid, out):
@@ -58,8 +58,8 @@ def tile_fastkanlayer_pa_kernel(tc, x, spline_weight, grid, out):
             psum_x = first.enter_context(tc.psum_pool(name="psum_x", bufs=8))
 
             x_clip = wide.tile([P, PACK, B], F32)
-            x_part = wide.tile([P, PACK, B], F32)
-            number = wide.tile([P, P, PACK], I32)
+            x_part = wide.tile([P, PACK // 2, B], F32)
+            minus_half = wide.tile([P, P], F32)
 
             clamp, dist, inner, outer = {}, {}, {}, {}
 
@@ -77,27 +77,30 @@ def tile_fastkanlayer_pa_kernel(tc, x, spline_weight, grid, out):
                         op1=ALU.min,
                     )
 
-            def turned_sum(parts, multiplied=()):
+            def turned_sum(parts, x_rows_part=None):
                 turned = psum_x.tile([P, PACK, P], F32, name="turned")
                 for t in range(PACK):
-                    for i, part in enumerate(parts):
+                    terms = [(part[:, t, :], identity, True) for part in parts]
+                    if x_rows_part is not None:
+                        if t % 2 == 0:
+                            terms.insert(0, (x_clip[:, t, x_rows_part], minus_half, False))
+                        else:
+                            terms.insert(0, (x_part[:, t // 2, x_rows_part], identity, True))
+                    for i, (part, turner, is_transpose) in enumerate(terms):
                         nc.tensor.matmul(
                             out=turned[:, t, :],
-                            lhsT=part[:, t, :],
-                            rhs=identity[:],
-                            is_transpose=(i > 0 or t not in multiplied),
+                            lhsT=part,
+                            rhs=turner[:],
+                            is_transpose=is_transpose,
                             start=(i == 0),
-                            stop=(i == len(parts) - 1),
+                            stop=(i == len(terms) - 1),
                         )
                 return turned
 
             def distance(n):
                 r, m = divmod(n, B_TILES)
                 dist[n] = act.tile([P, PACK, P], F32, name="dist", bufs=4)
-                wave = turned_sum(
-                    [x_part[:, :, m * P : (m + 1) * P]] + [clamp[n, k] for k in range(1, MEMBERS, 2)],
-                    multiplied=range(0, PACK, 2),
-                )
+                wave = turned_sum([clamp[n, k] for k in range(1, MEMBERS, 2)], slice(m * P, (m + 1) * P))
                 nc.scalar.activation(
                     out=dist[n][:], in_=wave[:], func=FUNC.Abs, bias=offset[:, r : r + 1], scale=-2.0
                 )
@@ -140,7 +143,8 @@ def tile_fastkanlayer_pa_kernel(tc, x, spline_weight, grid, out):
                 nc.vector.memset(warm[:], 0.0)
                 nc.scalar.activation(out=warm[:], in_=warm[:], func=FUNC.Abs)
                 x_rows = setup.tile([P, B_TILES, I], BF16)
-                nc.sync.dma_start(out=x_rows[:], in_=x.rearrange("(m r) i -> r m i", r=P))
+                for m in range(B_TILES):
+                    nc.sync.dma_start(out=x_rows[:, m, :], in_=x[m * P : (m + 1) * P, :])
                 grid_bf = setup.tile([P, C], BF16)
                 nc.sync.dma_start(out=grid_bf[:], in_=grid.partition_broadcast(P))
                 w_rows = spline_weight.rearrange("(p t) j c -> t p (j c)", t=PACK)
@@ -149,6 +153,75 @@ def tile_fastkanlayer_pa_kernel(tc, x, spline_weight, grid, out):
                 make_identity(nc, identity[:])
 
                 first.enter_context(tc.manual_schedule())
+                pairs = {}
+
+                def turn_x(m):
+                    pairs[m] = psum_x.tile([P, 2, P], F32, name="turned")
+                    words = x_rows[:, m, :].bitcast(F32).rearrange("r (p u) -> r u p", u=2)
+                    for u in range(2):
+                        nc.tensor.transpose(out=pairs[m][:, u, :], in_=words[:, u, :], identity=identity[:])
+
+                def clip_x(m):
+                    rows = slice(m * P, (m + 1) * P)
+                    nc.vector.tensor_scalar(
+                        out=x_clip[:, :, rows].rearrange("p (u e) b -> p u e b", e=2),
+                        in0=pairs[m][:]
+                        .rearrange("p u b -> p (u b)")
+                        .bitcast(BF16)
+                        .rearrange("p (u b e) -> p u e b", u=2, e=2),
+                        scalar1=0.99,
+                        scalar2=-0.99,
+                        op0=ALU.min,
+                        op1=ALU.max,
+                    )
+                    nc.scalar.activation(
+                        out=x_part[:, :, rows], in_=x_clip[:, 1:PACK:2, rows], func=FUNC.Copy, scale=-0.5
+                    )
+
+                def count(s, m):
+                    number[0] = act.tile([P, P, PACK], I32, name="number", bufs=2)
+                    nc.vector.tensor_scalar(
+                        out=number[0][:],
+                        in0=x_clip[:, :, m * P : (m + 1) * P].rearrange("p t b -> p b t"),
+                        scalar1=1.0 / (CLASSES * H),
+                        scalar2=(1.0 / H - s * SHARE + 3) / CLASSES + 0.5,
+                        op0=ALU.mult,
+                        op1=ALU.add,
+                    )
+
+                def to_member(s, m):
+                    to_rows = member[s][:, m * P : (m + 1) * P, :]
+                    if s % 2 == 0:
+                        nc.vector.tensor_copy(out=to_rows, in_=number[0][:])
+                    else:
+                        nc.scalar.activation(out=to_rows, in_=number[0][:].bitcast(U32), func=FUNC.Copy)
+
+                number = {}
+                counting = [(f, s, m) for m in range(B_TILES) for s in range(SETS) for f in (count, to_member)]
+
+                def unit_step(n):
+                    if 0 < n + 3 < B_TILES:
+                        clip_x(n + 3)
+                    if 0 <= n + 3 < units:
+                        clamps(n + 3)
+                    if 0 <= n + 1 < units:
+                        squares(n + 1)
+                    if 0 <= n + 2 < units:
+                        distance(n + 2)
+                    if 0 <= n < units:
+                        cubes(n)
+                        share = len(counting)
+                        for f, s, m in counting[n * share // units : (n + 1) * share // units]:
+                            f(s, m)
+                    if 0 <= n - 1 < units:
+                        combine(n - 1)
+
+                for m in range(B_TILES):
+                    turn_x(m)
+                clip_x(0)
+                nc.vector.tensor_scalar(
+                    out=minus_half[:], in0=identity[:], scalar1=-0.5, scalar2=None, op0=ALU.mult
+                )
                 nc.vector.tensor_scalar(
                     out=neg_grid[:], in0=grid_bf[:], scalar1=-1.0, scalar2=None, op0=ALU.mult
                 )
@@ -165,58 +238,6 @@ def tile_fastkanlayer_pa_kernel(tc, x, spline_weight, grid, out):
                     )
                     before = offset[:]
 
-                def load_x(m):
-                    rows = slice(m * P, (m + 1) * P)
-                    pairs = psum_x.tile([P, 2, P], F32, name="turned")
-                    words = x_rows[:, m, :].bitcast(F32).rearrange("r (p u) -> r u p", u=2)
-                    for u in range(2):
-                        nc.tensor.transpose(out=pairs[:, u, :], in_=words[:, u, :], identity=identity[:])
-                    nc.vector.tensor_scalar(
-                        out=x_clip[:, :, rows].rearrange("p (u e) b -> p u e b", e=2),
-                        in0=pairs[:]
-                        .rearrange("p u b -> p (u b)")
-                        .bitcast(BF16)
-                        .rearrange("p (u b e) -> p u e b", u=2, e=2),
-                        scalar1=0.99,
-                        scalar2=-0.99,
-                        op0=ALU.min,
-                        op1=ALU.max,
-                    )
-                    nc.scalar.activation(
-                        out=x_part[:, :, rows], in_=x_clip[:, :, rows], func=FUNC.Copy, scale=-0.5
-                    )
-
-                def count(s, m):
-                    nc.vector.tensor_scalar(
-                        out=number[:],
-                        in0=x_clip[:, :, m * P : (m + 1) * P].rearrange("p t b -> p b t"),
-                        scalar1=1.0 / (CLASSES * H),
-                        scalar2=(1.0 / H - s * SHARE + 3) / CLASSES + 0.5,
-                        op0=ALU.mult,
-                        op1=ALU.add,
-                    )
-
-                def to_member(s, m):
-                    nc.vector.tensor_copy(out=member[s][:, m * P : (m + 1) * P, :], in_=number[:])
-
-                counting = [(f, s, m) for s in range(SETS) for m in range(B_TILES) for f in (count, to_member)]
-
-                def unit_step(n):
-                    if 0 <= n + 3 < B_TILES:
-                        load_x(n + 3)
-                    if 0 <= n + 3 < units:
-                        clamps(n + 3)
-                    if 0 <= n + 2 < units:
-                        distance(n + 2)
-                    if 0 <= n + 1 < units:
-                        squares(n + 1)
-                    if 0 <= n < units:
-                        cubes(n)
-                        share = len(counting)
-                        for f, s, m in counting[n * share // units : (n + 1) * share // units]:
-                            f(s, m)
-                    if 0 <= n - 1 < units:
-                        combine(n - 1)
 
                 for n in range(-3, EARLY * B_TILES):
                     unit_step(n)
@@ -245,7 +266,8 @@ def tile_fastkanlayer_pa_kernel(tc, x, spline_weight, grid, out):
                 grouped[g] = groups.tile([P, GROUP, J, PACK], BF16, name="grouped", align_bytes=64)
                 for piece in range(PIECES):
                     js = slice(piece * J_PIECE, (piece + 1) * J_PIECE)
-                    nc.scalar.copy(
+                    on_vector = g == 0 and piece >= PIECES // 2
+                    (nc.vector.tensor_copy if on_vector else nc.scalar.copy)(
                         out=grouped[g][:, 0:count_c, js, :].rearrange("p c j t -> p j t c"),
                         in_=w_view[:, js, :, first_c : first_c + count_c],
                     )

@@ -28,6 +28,7 @@ CLASSES = 7
 MEMBERS = C // CLASSES
 SHARE = 2
 SETS = -(-CLASSES // SHARE)
+CENTRE = MEMBERS // 2
 EARLY = 4
 
 GROUP = 3
@@ -178,26 +179,67 @@ def tile_fastkanlayer_pa_kernel(tc, x, spline_weight, grid, out):
                         out=x_part[:, :, rows], in_=x_clip[:, 1:PACK:2, rows], func=FUNC.Copy, scale=-0.5
                     )
 
-                def count(s, m):
-                    number[0] = act.tile([P, P, PACK], I32, name="number", bufs=2)
+                def count(m):
+                    number[0] = act.tile([P, P, PACK], I32, name="number", bufs=1)
                     nc.vector.tensor_scalar(
                         out=number[0][:],
                         in0=x_clip[:, :, m * P : (m + 1) * P].rearrange("p t b -> p b t"),
                         scalar1=1.0 / (CLASSES * H),
-                        scalar2=(1.0 / H - s * SHARE + 3) / CLASSES + 0.5,
+                        scalar2=(1.0 / H + 3) / CLASSES - 0.5,
                         op0=ALU.mult,
                         op1=ALU.add,
                     )
 
-                def to_member(s, m):
-                    to_rows = member[s][:, m * P : (m + 1) * P, :]
-                    if s % 2 == 0:
-                        nc.vector.tensor_copy(out=to_rows, in_=number[0][:])
-                    else:
-                        nc.scalar.activation(out=to_rows, in_=number[0][:].bitcast(U32), func=FUNC.Copy)
+                def rows_of(s, m):
+                    return member[s][:, m * P : (m + 1) * P, :]
 
-                number = {}
-                counting = [(f, s, m) for m in range(B_TILES) for s in range(SETS) for f in (count, to_member)]
+                def to_member(m):
+                    nc.scalar.activation(
+                        out=rows_of(0, m), in_=number[0][:].bitcast(U32), func=FUNC.Copy, bias=-float(CENTRE)
+                    )
+
+                def beyond(m):
+                    past[0] = act.tile([P, P, PACK], BF16, name="past", bufs=1)
+                    nc.vector.scalar_tensor_tensor(
+                        out=past[0][:],
+                        in0=rows_of(0, m),
+                        scalar=-CLASSES * H,
+                        in1=x_clip[:, :, m * P : (m + 1) * P].rearrange("p t b -> p b t"),
+                        op0=ALU.mult,
+                        op1=ALU.add,
+                    )
+
+                def short(s, m):
+                    less[s] = act.tile([P, P, PACK], BF16, name="less", bufs=2)
+                    nc.vector.tensor_scalar(
+                        out=less[s][:],
+                        in0=past[0][:],
+                        scalar1=-1.0 + H * (CLASSES * CENTRE - 3 + s * SHARE),
+                        scalar2=None,
+                        op0=ALU.is_lt,
+                    )
+
+                def to_set(s, m):
+                    nc.vector.tensor_tensor(
+                        out=rows_of(s, m), in0=rows_of(0, m), in1=less[s][:], op=ALU.subtract
+                    )
+
+                number, past, less = {}, {}, {}
+
+                def counting(n):
+                    m, step = divmod(n * B_TILES, units)
+                    step //= B_TILES
+                    if step == 0:
+                        count(m)
+                    elif step == 1:
+                        to_member(m)
+                    elif step == 2:
+                        beyond(m)
+                    else:
+                        if step > 3:
+                            to_set(step - 3, m)
+                        if step < 3 + SETS - 1:
+                            short(step - 2, m)
 
                 def unit_step(n):
                     if 0 < n + 3 < B_TILES:
@@ -210,9 +252,7 @@ def tile_fastkanlayer_pa_kernel(tc, x, spline_weight, grid, out):
                         distance(n + 2)
                     if 0 <= n < units:
                         cubes(n)
-                        share = len(counting)
-                        for f, s, m in counting[n * share // units : (n + 1) * share // units]:
-                            f(s, m)
+                        counting(n)
                     if 0 <= n - 1 < units:
                         combine(n - 1)
 
@@ -280,7 +320,7 @@ def tile_fastkanlayer_pa_kernel(tc, x, spline_weight, grid, out):
                     nc.vector.tensor_scalar(
                         out=mask[s, k][:],
                         in0=member[s][:].rearrange("p b t -> p (b t)"),
-                        scalar1=float(k + 1),
+                        scalar1=float(k - CENTRE),
                         scalar2=None,
                         op0=ALU.is_equal,
                     )

import math
from contextlib import ExitStack

import concourse.mybir as mybir
from concourse.masks import make_identity

F32 = mybir.dt.float32
BF16 = mybir.dt.bfloat16
I32 = mybir.dt.int32
U32 = mybir.dt.uint32
U8 = mybir.dt.uint8
FP8X4 = mybir.dt.float8_e4m3fn_x4
FUNC = mybir.ActivationFunctionType
ALU = mybir.AluOpType

P = 128
PACK = 4
B, I, J, C = 512, 512, 512, 35
B_TILES = B // P
FLOPS = 2 * B * J * C * I

H = 2.0 / (C - 1)
REACH = 2.0 * H
OUTER_SCALE = 1.0 / math.sqrt(6.0 * H**3)
INNER_SCALE = math.sqrt(2.0 / (3.0 * H**3))

CLASSES = 7
MEMBERS = C // CLASSES
SHARE = 2
SETS = -(-CLASSES // SHARE)
CENTRE = MEMBERS // 2
EARLY = 4

GROUP = 3
STARTS = [0] + list(range(2, C, GROUP))
PIECES = 4
J_PIECE = J // PIECES
LAG = 4


def tile_fastkanlayer_pa_kernel(tc, x, spline_weight, grid, out):
    nc = tc.nc
    with ExitStack() as ctx:
        keep = ctx.enter_context(tc.tile_pool(name="keep", bufs=1, side="left"))

        w_raw = keep.tile([P, PACK, J * C], BF16)
        neg_grid = keep.tile([P, C], F32)
        sums = keep.tile([P, C], F32)
        mids = keep.tile([P, C], F32)
        offset = keep.tile([P, CLASSES], F32)
        identity = keep.tile([P, P], F32)
        member = [keep.tile([P, B, PACK], BF16, name="member%d" % s) for s in range(SETS)]
        value = [keep.tile([P, B, PACK], BF16, name="value%d" % r) for r in range(EARLY)]

        with ExitStack() as first:
            wide = first.enter_context(tc.tile_pool(name="wide", bufs=1, side="right"))
            clamp_pool = first.enter_context(tc.tile_pool(name="clamp_pool", bufs=8, side="right"))
            act = first.enter_context(tc.tile_pool(name="act", bufs=3, side="right"))
            psum_x = first.enter_context(tc.psum_pool(name="psum_x", bufs=8))

            x_clip = wide.tile([P, PACK, B], F32)
            x_part = wide.tile([P, PACK // 2, B], F32)
            minus_half = wide.tile([P, P], F32)

            clamp, dist, inner, outer = {}, {}, {}, {}

            def clamps(n):
                r, m = divmod(n, B_TILES)
                for k in range(1, MEMBERS, 2):
                    c = r + CLASSES * k
                    clamp[n, k] = clamp_pool.tile([P, PACK, P], F32, name="clamp")
                    nc.vector.tensor_scalar(
                        out=clamp[n, k][:],
                        in0=x_clip[:, :, m * P : (m + 1) * P],
                        scalar1=mids[:, c : c + 1],
                        scalar2=mids[:, c + CLASSES : c + CLASSES + 1],
                        op0=ALU.max,
                        op1=ALU.min,
                    )

            def turned_sum(parts, x_rows_part=None):
                turned = psum_x.tile([P, PACK, P], F32, name="turned")
                for t in range(PACK):
                    terms = [(part[:, t, :], identity, True) for part in parts]
                    if x_rows_part is not None:
                        if t % 2 == 0:
                            terms.insert(0, (x_clip[:, t, x_rows_part], minus_half, False))
                        else:
                            terms.insert(0, (x_part[:, t // 2, x_rows_part], identity, True))
                    for i, (part, turner, is_transpose) in enumerate(terms):
                        nc.tensor.matmul(
                            out=turned[:, t, :],
                            lhsT=part,
                            rhs=turner[:],
                            is_transpose=is_transpose,
                            start=(i == 0),
                            stop=(i == len(terms) - 1),
                        )
                return turned

            def distance(n):
                r, m = divmod(n, B_TILES)
                dist[n] = act.tile([P, PACK, P], F32, name="dist", bufs=4)
                wave = turned_sum([clamp[n, k] for k in range(1, MEMBERS, 2)], slice(m * P, (m + 1) * P))
                nc.scalar.activation(
                    out=dist[n][:], in_=wave[:], func=FUNC.Abs, bias=offset[:, r : r + 1], scale=-2.0
                )

            def squares(n):
                inner[n] = act.tile([P, PACK, P], F32, name="inner")
                nc.scalar.activation(
                    out=inner[n][:], in_=dist[n][:], func=FUNC.Square, bias=INNER_SCALE * H, scale=-INNER_SCALE
                )
                outer[n] = act.tile([P, PACK, P], F32, name="outer")
                nc.scalar.activation(
                    out=outer[n][:], in_=dist[n][:], func=FUNC.Square, bias=OUTER_SCALE * REACH, scale=-OUTER_SCALE
                )

            def cubes(n):
                nc.vector.scalar_tensor_tensor(
                    out=inner[n][:], in0=dist[n][:], scalar=H, in1=inner[n][:], op0=ALU.subtract, op1=ALU.mult
                )
                nc.vector.scalar_tensor_tensor(
                    out=outer[n][:], in0=dist[n][:], scalar=REACH, in1=outer[n][:], op0=ALU.subtract, op1=ALU.mult
                )
                nc.vector.tensor_scalar(
                    out=inner[n][:], in0=inner[n][:], scalar1=-1.0, scalar2=0.0, op0=ALU.mult, op1=ALU.max
                )

            def combine(n):
                r, m = divmod(n, B_TILES)
                minus = turned_sum([outer[n], inner[n]])
                nc.scalar.activation(
                    out=value[r][:, m * P : (m + 1) * P, :],
                    in_=minus[:].rearrange("p t b -> p b t"),
                    func=FUNC.Relu,
                    scale=-1.0,
                )

            units = CLASSES * B_TILES

            with tc.tile_pool(name="setup", bufs=1, side="left") as setup:
                warm = setup.tile([P, 1], F32)
                nc.vector.memset(warm[:], 0.0)
                nc.scalar.activation(out=warm[:], in_=warm[:], func=FUNC.Abs)
                x_rows = setup.tile([P, B_TILES, I], BF16)
                for m in range(B_TILES):
                    nc.sync.dma_start(out=x_rows[:, m, :], in_=x[m * P : (m + 1) * P, :])
                grid_bf = setup.tile([P, C], BF16)
                nc.sync.dma_start(out=grid_bf[:], in_=grid.partition_broadcast(P))
                w_rows = spline_weight.rearrange("(p t) j c -> t p (j c)", t=PACK)
                for t in range(PACK):
                    nc.sync.dma_start(out=w_raw[:, t, :], in_=w_rows[t])
                make_identity(nc, identity[:])

                first.enter_context(tc.manual_schedule())
                pairs = {}

                def turn_x(m):
                    pairs[m] = psum_x.tile([P, 2, P], F32, name="turned")
                    words = x_rows[:, m, :].bitcast(F32).rearrange("r (p u) -> r u p", u=2)
                    for u in range(2):
                        nc.tensor.transpose(out=pairs[m][:, u, :], in_=words[:, u, :], identity=identity[:])

                def clip_x(m):
                    rows = slice(m * P, (m + 1) * P)
                    nc.vector.tensor_scalar(
                        out=x_clip[:, :, rows].rearrange("p (u e) b -> p u e b", e=2),
                        in0=pairs[m][:]
                        .rearrange("p u b -> p (u b)")
                        .bitcast(BF16)
                        .rearrange("p (u b e) -> p u e b", u=2, e=2),
                        scalar1=0.99,
                        scalar2=-0.99,
                        op0=ALU.min,
                        op1=ALU.max,
                    )
                    nc.scalar.activation(
                        out=x_part[:, :, rows], in_=x_clip[:, 1:PACK:2, rows], func=FUNC.Copy, scale=-0.5
                    )

                def count(m):
                    number[0] = act.tile([P, P, PACK], I32, name="number", bufs=1)
                    nc.vector.tensor_scalar(
                        out=number[0][:],
                        in0=x_clip[:, :, m * P : (m + 1) * P].rearrange("p t b -> p b t"),
                        scalar1=1.0 / (CLASSES * H),
                        scalar2=(1.0 / H + 3) / CLASSES - 0.5,
                        op0=ALU.mult,
                        op1=ALU.add,
                    )

                def rows_of(s, m):
                    return member[s][:, m * P : (m + 1) * P, :]

                def to_member(m):
                    nc.scalar.activation(
                        out=rows_of(0, m), in_=number[0][:].bitcast(U32), func=FUNC.Copy, bias=-float(CENTRE)
                    )

                def beyond(m):
                    past[0] = act.tile([P, P, PACK], BF16, name="past", bufs=1)
                    nc.vector.scalar_tensor_tensor(
                        out=past[0][:],
                        in0=rows_of(0, m),
                        scalar=-CLASSES * H,
                        in1=x_clip[:, :, m * P : (m + 1) * P].rearrange("p t b -> p b t"),
                        op0=ALU.mult,
                        op1=ALU.add,
                    )

                def short(s, m):
                    less[s] = act.tile([P, P, PACK], BF16, name="less", bufs=2)
                    nc.vector.tensor_scalar(
                        out=less[s][:],
                        in0=past[0][:],
                        scalar1=-1.0 + H * (CLASSES * CENTRE - 3 + s * SHARE),
                        scalar2=None,
                        op0=ALU.is_lt,
                    )

                def to_set(s, m):
                    nc.vector.tensor_tensor(
                        out=rows_of(s, m), in0=rows_of(0, m), in1=less[s][:], op=ALU.subtract
                    )

                number, past, less = {}, {}, {}

                def counting(n):
                    m, step = divmod(n * B_TILES, units)
                    step //= B_TILES
                    if step == 0:
                        count(m)
                    elif step == 1:
                        to_member(m)
                    elif step == 2:
                        beyond(m)
                    else:
                        if step > 3:
                            to_set(step - 3, m)
                        if step < 3 + SETS - 1:
                            short(step - 2, m)

                def unit_step(n):
                    if 0 < n + 3 < B_TILES:
                        clip_x(n + 3)
                    if 0 <= n + 3 < units:
                        clamps(n + 3)
                    if 0 <= n + 1 < units:
                        squares(n + 1)
                    if 0 <= n + 2 < units:
                        distance(n + 2)
                    if 0 <= n < units:
                        cubes(n)
                        counting(n)
                    if 0 <= n - 1 < units:
                        combine(n - 1)

                for m in range(B_TILES):
                    turn_x(m)
                clip_x(0)
                nc.vector.tensor_scalar(
                    out=minus_half[:], in0=identity[:], scalar1=-0.5, scalar2=None, op0=ALU.mult
                )
                nc.vector.tensor_scalar(
                    out=neg_grid[:], in0=grid_bf[:], scalar1=-1.0, scalar2=None, op0=ALU.mult
                )
                nc.vector.tensor_tensor(
                    out=sums[:, CLASSES:C], in0=grid_bf[:, 0 : C - CLASSES], in1=grid_bf[:, CLASSES:C], op=ALU.add
                )
                nc.vector.tensor_scalar(
                    out=mids[:, CLASSES:C], in0=sums[:, CLASSES:C], scalar1=0.5, scalar2=None, op0=ALU.mult
                )
                before = neg_grid[:, 0:CLASSES]
                for k in range(1, MEMBERS, 2):
                    nc.vector.tensor_tensor(
                        out=offset[:], in0=before, in1=sums[:, k * CLASSES : (k + 1) * CLASSES], op=ALU.add
                    )
                    before = offset[:]


                for n in range(-3, EARLY * B_TILES):
                    unit_step(n)

            late = ctx.enter_context(tc.tile_pool(name="late", bufs=1, side="left"))
            value.extend([late.tile([P, B, PACK], BF16, name="value%d" % r) for r in range(EARLY, CLASSES)])
            for n in range(EARLY * B_TILES, units + 1):
                unit_step(n)

        psum_acc = ctx.enter_context(tc.psum_pool(name="psum_acc", bufs=1))
        acc = [psum_acc.tile([P, J], F32, name="acc%d" % m) for m in range(B_TILES)]
        w_view = w_raw[:].rearrange("p t (j c) -> p j t c", c=C)

        with ExitStack() as second:
            groups = second.enter_context(tc.tile_pool(name="groups", bufs=2, side="right"))
            stage = second.enter_context(tc.tile_pool(name="stage", bufs=2, side="right"))
            second.enter_context(tc.manual_schedule())

            mask, basis, b_codes, b_scales, grouped, w_codes, w_scales, place = {}, {}, {}, {}, {}, {}, {}, {}

            def regroup(g):
                first_c = STARTS[g]
                count_c = (STARTS + [C])[g + 1] - first_c
                for c in range(first_c, first_c + count_c):
                    place[c] = (g, c - first_c)
                grouped[g] = groups.tile([P, GROUP, J, PACK], BF16, name="grouped", align_bytes=64)
                for piece in range(PIECES):
                    js = slice(piece * J_PIECE, (piece + 1) * J_PIECE)
                    on_vector = g == 0 and piece >= PIECES // 2
                    (nc.vector.tensor_copy if on_vector else nc.scalar.copy)(
                        out=grouped[g][:, 0:count_c, js, :].rearrange("p c j t -> p j t c"),
                        in_=w_view[:, js, :, first_c : first_c + count_c],
                    )

            def make_mask(c):
                r, k = c % CLASSES, c // CLASSES
                s = r // SHARE
                if r % SHARE == 0:
                    mask[s, k] = stage.tile([P, B * PACK], BF16, name="mask", bufs=1)
                    nc.vector.tensor_scalar(
                        out=mask[s, k][:],
                        in0=member[s][:].rearrange("p b t -> p (b t)"),
                        scalar1=float(k - CENTRE),
                        scalar2=None,
                        op0=ALU.is_equal,
                    )

            def expand(c):
                r, k = c % CLASSES, c // CLASSES
                basis[c] = stage.tile([P, B * PACK], BF16, name="basis", align_bytes=64)
                nc.vector.tensor_tensor(
                    out=basis[c][:],
                    in0=value[r][:].rearrange("p b t -> p (b t)"),
                    in1=mask[r // SHARE, k][:],
                    op=ALU.mult,
                )

            def quantise_basis(c):
                b_codes[c] = stage.tile([P, B], U32, name="b_codes", bufs=LAG + 1, align_bytes=64)
                b_scales[c] = stage.tile([P, B], U8, name="b_scales", bufs=LAG + 1, align_bytes=64)
                nc.vector.quantize_mx(out=b_codes[c][:].bitcast(FP8X4), scales=b_scales[c][:], in_=basis[c][:])

            def quantise_weights(c):
                w_codes[c] = stage.tile([P, J], U32, name="w_codes", align_bytes=64)
                w_scales[c] = stage.tile([P, J], U8, name="w_scales", align_bytes=64)
                nc.vector.quantize_mx(
                    out=w_codes[c][:].bitcast(FP8X4),
                    scales=w_scales[c][:],
                    in_=grouped[place[c][0]][:, place[c][1], :, :].rearrange("p j t -> p (j t)"),
                )

            def multiply(c):
                for m in range(B_TILES):
                    rows = slice(m * P, (m + 1) * P)
                    nc.tensor.matmul_mx(
                        out=acc[m][:],
                        lhsT=b_codes[c][:, rows].bitcast(FP8X4),
                        lhsT_scale=b_scales[c][:, rows],
                        rhs=w_codes[c][:].bitcast(FP8X4),
                        rhs_scale=w_scales[c][:],
                        start=(c == 0),
                        stop=(c == C - 1),
                    )

            regroup(0)
            for c in range(C + LAG):
                w = c - LAG
                if w in STARTS[:-1]:
                    regroup(STARTS.index(w) + 1)
                if c < C:
                    make_mask(c)
                if w >= 0:
                    quantise_weights(w)
                if c < C:
                    expand(c)
                if 1 <= c <= C:
                    quantise_basis(c - 1)
                if w >= 0:
                    multiply(w)

        with tc.tile_pool(name="result", bufs=B_TILES, side="right") as result:
            for m in range(B_TILES):
                out_rows = result.tile([P, J], F32)
                if m % 2 == 0:
                    nc.scalar.copy(out=out_rows[:], in_=acc[m][:])
                else:
                    nc.vector.tensor_copy(out=out_rows[:], in_=acc[m][:])
                nc.sync.dma_start(out=out[m * P : (m + 1) * P, :], in_=out_rows[:])
